import numpy as np
import ml_dtypes


def mxq(x, axis, fmt="e4m3"):
    dtype, down = {"e4m3": (ml_dtypes.float8_e4m3fn, 7), "e5m2": (ml_dtypes.float8_e5m2, 14)}[fmt]
    v = np.moveaxis(np.asarray(x, np.float32).astype(ml_dtypes.bfloat16).astype(np.float64), axis, -1)
    blocks = v.reshape(v.shape[:-1] + (-1, 32))
    amax = np.abs(blocks).max(-1, keepdims=True)
    byte = np.maximum(np.where(amax > 0, np.frexp(amax)[1] - 1 + 127, 0) - down, 1)
    scale = np.exp2(byte - 127.0)
    codes = (blocks / scale).astype(np.float32).astype(dtype).astype(np.float64)
    return np.moveaxis((codes * scale).reshape(v.shape), -1, axis)


WIDE = False


def mx_kscale(k):
    if not WIDE:
        return np.ones(k)
    levels = np.array([10, -10, 5, -5, 0])
    a = np.random.permutation(np.resize(levels, k // 512 * 4)).reshape(k // 512, 4)
    idx = np.arange(k)
    return np.exp2(a[idx // 512, idx % 128 // 32])


BF16 = ml_dtypes.bfloat16


def bf(x):
    return np.asarray(x, np.float32).astype(BF16)


def f64(x):
    return np.asarray(x).astype(np.float64)


B, C, H, W, HEADS, HD = 16, 512, 16, 16, 2, 512
N = H * W


def setup_inputs():
    t = mx_kscale(HD)
    return {"x": bf(np.random.standard_normal((B, C, H, W))),
            "q_w": bf(np.random.standard_normal((HEADS, HD, C)) * 0.5 / np.sqrt(C) * t[None, :, None]),
            "q_b": bf(np.random.standard_normal((HEADS, HD)) * 4.0 / N * t),
            "k_w": bf(np.random.standard_normal((HEADS, HD, C)) * 0.5 / np.sqrt(C) / t[None, :, None]),
            "k_b": bf(np.random.standard_normal((HEADS, HD)) * 0.1 / t)}


def reference(x, q_w, q_b, k_w, k_b):
    x = f64(x)
    patch = x.transpose(0, 2, 3, 1).reshape(B, N, C)
    pq = mxq(patch, 2, "e4m3")[:, None]
    Q = (pq @ mxq(f64(q_w), 2, "e4m3").transpose(0, 2, 1)[None]) + f64(q_b)[None, :, None, :]
    K = (pq @ mxq(f64(k_w), 2, "e4m3").transpose(0, 2, 1)[None]) + f64(k_b)[None, :, None, :]
    sim = (mxq(Q, 3, "e4m3") @ mxq(K, 3, "e4m3").transpose(0, 1, 3, 2)) / np.sqrt(HD)
    att = sim.sum(axis=2)[:, :, None, :]
    e = np.exp(att - att.max(axis=1, keepdims=True))
    att = e / e.sum(axis=1, keepdims=True)
    attention_score = att.reshape(B, HEADS, H, W)
    x_enhance = (attention_score[:, :, None, :, :] * x[:, None, :, :, :]).reshape(B, HEADS * C, H, W)
    return (attention_score, x_enhance, sim)

@@ -1,0 +1,198 @@
+import math
+
+import concourse.bass as bass
+import concourse.mybir as mybir
+import concourse.tile as tile
+from concourse.masks import make_identity
+
+F32 = mybir.dt.float32
+BF16 = mybir.dt.bfloat16
+U32 = mybir.dt.uint32
+U8 = mybir.dt.uint8
+FP8X4 = mybir.dt.float8_e4m3fn_x4
+ACT = mybir.ActivationFunctionType
+ALU = mybir.AluOpType
+
+P = 128
+B, C, N, HEADS, HD = 16, 512, 256, 2, 512
+PACK = 4
+FLOPS = 2 * B * HEADS * 2 * N * C * HD + 2 * B * HEADS * N * N * HD
+
+VECTOR_PRODUCTS = ((15, 0), (15, 1))
+
+
+def tile_acd_pa_t_kernel(tc, x, q_w, q_b, k_w, k_b, out_0, out_1, out_2):
+    nc = tc.nc
+    inv_sqrt = 1.0 / math.sqrt(HD)
+    with tc.tile_pool(name="const", bufs=1) as const, tc.tile_pool(name="work", bufs=2) as work, tc.psum_pool(
+        name="psum", bufs=2
+    ) as psum:
+        w_dram = (q_w[0], k_w[0], q_w[1], k_w[1])
+        w_raw = [const.tile([P, PACK, C], BF16, name="w_raw%d" % m) for m in range(4)]
+        x_raw = [const.tile([P, 2, PACK, N], BF16, name="x_raw%d" % bp) for bp in range(B // 2)]
+
+        def load_w(m):
+            nc.sync.dma_start(
+                out=w_raw[m][:].rearrange("p t c -> p (t c)"),
+                in_=w_dram[m].rearrange("(p t) c -> p (t c)", t=PACK),
+            )
+
+        def load_x(bp):
+            nc.sync.dma_start(
+                out=x_raw[bp][:].rearrange("p b j n -> p b (j n)"),
+                in_=x[2 * bp : 2 * bp + 2].rearrange("b (p j) h w -> p b (j h w)", j=PACK),
+            )
+
+        qb_bf = const.tile([P, HEADS, PACK], BF16, name="qb_bf")
+        kb_bf = const.tile([P, HEADS, PACK], BF16, name="kb_bf")
+        load_w(0)
+        load_x(0)
+        load_w(1)
+        with nc.allow_non_contiguous_dma(reason="bias: four neighbouring values to a partition"):
+            nc.sync.dma_start(out=qb_bf[:], in_=q_b.rearrange("h (p t) -> p h t", t=PACK))
+            nc.sync.dma_start(out=kb_bf[:], in_=k_b.rearrange("h (p t) -> p h t", t=PACK))
+        load_w(2)
+        load_w(3)
+        for bp in range(1, B // 2):
+            load_x(bp)
+
+        ident = const.tile([P, P], F32, name="ident")
+        make_identity(nc, ident[:])
+        ones_pos = const.tile([P, P], F32, name="ones_pos")
+        ones_neg = const.tile([P, P], F32, name="ones_neg")
+        nc.vector.memset(ones_pos[:], 1.0)
+        nc.vector.memset(ones_neg[:], -1.0)
+        warm_in = const.tile([P, 1], F32, name="warm_in")
+        warm_out = const.tile([P, 1], F32, name="warm_out")
+        nc.vector.memset(warm_in[:], 0.0)
+        nc.scalar.activation(out=warm_out[:], in_=warm_in[:], func=ACT.Sigmoid)
+        bias_f = const.tile([P, HEADS, 2, PACK], F32, name="bias_f")
+        nc.vector.tensor_copy(out=bias_f[:, :, 0, :], in_=qb_bf[:])
+        nc.vector.tensor_copy(out=bias_f[:, :, 1, :], in_=kb_bf[:])
+
+        w_codes = [const.tile([P, HD], U32, name="w_codes%d" % m, align_bytes=64) for m in range(4)]
+        w_scales = [const.tile([P, HD], U8, name="w_scales%d" % m, align_bytes=64) for m in range(4)]
+
+        def prepare_w(m):
+            words = w_raw[m][:].bitcast(F32)
+            w_grouped = work.tile([P, PACK, P, PACK], BF16, name="w_grouped", align_bytes=64)
+            grouped_words = w_grouped[:].bitcast(F32)
+            for half in range(2):
+                bank = psum.tile([P, 2, 2, P], F32, name="w_bank", tag="qk", bufs=4)
+                for tt in range(2):
+                    for u in range(2):
+                        nc.tensor.transpose(bank[:, tt, u, :], words[:, 2 * half + tt, u : C // 2 : 2], ident[:])
+                dst = grouped_words[:, 2 * half : 2 * half + 2, :, :]
+                src = bank[:].rearrange("p t u d -> p t d u")
+                if half == 0:
+                    nc.vector.tensor_copy(out=dst, in_=src)
+                else:
+                    nc.scalar.copy(out=dst, in_=src)
+            nc.vector.quantize_mx(
+                out=w_codes[m][:].bitcast(FP8X4),
+                scales=w_scales[m][:],
+                in_=w_grouped[:].rearrange("p t d j -> p (t d j)"),
+            )
+
+        def prepare_x(bp):
+            x_grouped = work.tile([P, 2, N, PACK], BF16, name="x_grouped", align_bytes=64)
+            for b2 in range(2):
+                nc.scalar.copy(
+                    out=x_grouped[:, b2].rearrange("p (c i) t -> p c t i", i=4),
+                    in_=x_raw[bp][:, b2].rearrange("p t (c i) -> p c t i", i=4),
+                )
+            x_codes = work.tile([P, 2 * N], U32, name="x_codes", align_bytes=64)
+            x_scales = work.tile([P, 2 * N], U8, name="x_scales", align_bytes=64)
+            nc.vector.quantize_mx(
+                out=x_codes[:].bitcast(FP8X4),
+                scales=x_scales[:],
+                in_=x_grouped[:].rearrange("p b n j -> p (b n j)"),
+            )
+            return x_codes, x_scales
+
+        prepare_w(0)
+        xq = prepare_x(0)
+        prepare_w(1)
+        prepare_w(2)
+        prepare_w(3)
+
+        for bp in range(B // 2):
+            x_codes, x_scales = xq
+            for b2 in range(2):
+                b = 2 * bp + b2
+                sim_sb = work.tile([P, HEADS, 2, N], F32, name="sim_sb", bufs=3)
+                for h in range(HEADS):
+                    qk_grouped = work.tile([P, 2, N, PACK], BF16, name="qk_grouped", bufs=4, align_bytes=64)
+                    for qk in range(2):
+                        m = 2 * h + qk
+                        for nh in range(2):
+                            bank = psum.tile([P, PACK, P], F32, name="qk_bank", tag="qk", bufs=4)
+                            cols = slice(b2 * N + nh * P, b2 * N + (nh + 1) * P)
+                            for t in range(PACK):
+                                nc.tensor.matmul_mx(
+                                    out=bank[:, t, :],
+                                    lhsT=w_codes[m][:, t * P : (t + 1) * P].bitcast(FP8X4),
+                                    lhsT_scale=w_scales[m][:, t * P : (t + 1) * P],
+                                    rhs=x_codes[:, cols].bitcast(FP8X4),
+                                    rhs_scale=x_scales[:, cols],
+                                    start=True,
+                                    stop=True,
+                                )
+                            nc.vector.tensor_tensor(
+                                out=qk_grouped[:, qk, nh * P : (nh + 1) * P, :],
+                                in0=bank[:].rearrange("p t c -> p c t"),
+                                in1=bias_f[:, h, qk, :].unsqueeze(1).to_broadcast([P, P, PACK]),
+                                op=ALU.add,
+                            )
+                    qk_codes = work.tile([P, 2 * N], U32, name="qk_codes", bufs=3, align_bytes=64)
+                    qk_scales = work.tile([P, 2 * N], U8, name="qk_scales", bufs=3, align_bytes=64)
+                    nc.vector.quantize_mx(
+                        out=qk_codes[:].bitcast(FP8X4),
+                        scales=qk_scales[:],
+                        in_=qk_grouped[:].rearrange("p a n j -> p (a n j)"),
+                    )
+                    sim_bank = psum.tile([P, 2, N], F32, name="sim_bank", tag="sim", bufs=2)
+                    for qt in range(2):
+                        nc.tensor.matmul_mx(
+                            out=sim_bank[:, qt, :],
+                            lhsT=qk_codes[:, qt * P : (qt + 1) * P].bitcast(FP8X4),
+                            lhsT_scale=qk_scales[:, qt * P : (qt + 1) * P],
+                            rhs=qk_codes[:, N : 2 * N].bitcast(FP8X4),
+                            rhs_scale=qk_scales[:, N : 2 * N],
+                            start=True,
+                            stop=True,
+                        )
+                    nc.scalar.activation(out=sim_sb[:, h], in_=sim_bank[:], func=ACT.Copy, scale=inv_sqrt)
+                nc.sync.dma_start(
+                    out=out_2[b].rearrange("h (qt p) k -> p (h qt) k", p=P),
+                    in_=sim_sb[:].rearrange("p h qt k -> p (h qt) k"),
+                )
+                diff = psum.tile([P, N], F32, name="diff", tag="diff", bufs=2)
+                for h in range(HEADS):
+                    for qt in range(2):
+                        nc.tensor.matmul(
+                            out=diff[:],
+                            lhsT=(ones_pos if h == 0 else ones_neg)[:],
+                            rhs=sim_sb[:, h, qt, :],
+                            start=(h == 0 and qt == 0),
+                            stop=(h == 1 and qt == 1),
+                        )
+                att = work.tile([P, HEADS, N], F32, name="att", bufs=3)
+                nc.scalar.activation(out=att[:, 0, :], in_=diff[:], func=ACT.Sigmoid)
+                nc.scalar.activation(out=att[:, 1, :], in_=diff[:], func=ACT.Sigmoid, scale=-1.0)
+                nc.sync.dma_start(out=out_0[b : b + 1].rearrange("o h i j -> o h (i j)"), in_=att[0:1, :, :])
+                enhanced = work.tile([P, HEADS, PACK, N], F32, name="enhanced", bufs=4)
+                for h in range(HEADS):
+                    engine = nc.vector if (b, h) in VECTOR_PRODUCTS else nc.gpsimd
+                    engine.tensor_tensor(
+                        out=enhanced[:, h],
+                        in0=x_raw[bp][:, b2],
+                        in1=att[:, h, :].unsqueeze(1).to_broadcast([P, PACK, N]),
+                        op=ALU.mult,
+                    )
+                nc.sync.dma_start(
+                    out=out_1[b].rearrange("(h p j) i w -> p h (j i w)", h=HEADS, j=PACK),
+                    in_=enhanced[:].rearrange("p h j n -> p h (j n)"),
+                )
+                if b2 == 0 and bp + 1 < B // 2:
+                    xq = prepare_x(bp + 1)

@@ -1,8 +1,7 @@
 import math
+from contextlib import ExitStack
 
-import concourse.bass as bass
 import concourse.mybir as mybir
-import concourse.tile as tile
 from concourse.masks import make_identity
 
 F32 = mybir.dt.float32
@@ -17,19 +16,23 @@ P = 128
 B, C, N, HEADS, HD = 16, 512, 256, 2, 512
 PACK = 4
 FLOPS = 2 * B * HEADS * 2 * N * C * HD + 2 * B * HEADS * N * N * HD
-
-VECTOR_PRODUCTS = ((15, 0), (15, 1))
+VECTOR_BATCHES = (14, 15)
 
 
 def tile_acd_pa_t_kernel(tc, x, q_w, q_b, k_w, k_b, out_0, out_1, out_2):
     nc = tc.nc
     inv_sqrt = 1.0 / math.sqrt(HD)
-    with tc.tile_pool(name="const", bufs=1) as const, tc.tile_pool(name="work", bufs=2) as work, tc.psum_pool(
-        name="psum", bufs=2
-    ) as psum:
+    with ExitStack() as ctx:
+        const = ctx.enter_context(tc.tile_pool(name="const", bufs=1))
+        work = ctx.enter_context(tc.tile_pool(name="work", bufs=2))
+        psum = ctx.enter_context(tc.psum_pool(name="psum", bufs=1))
+        ctx.enter_context(tc.manual_schedule())
+
         w_dram = (q_w[0], k_w[0], q_w[1], k_w[1])
         w_raw = [const.tile([P, PACK, C], BF16, name="w_raw%d" % m) for m in range(4)]
-        x_raw = [const.tile([P, 2, PACK, N], BF16, name="x_raw%d" % bp) for bp in range(B // 2)]
+        x_raw = [const.tile([P, PACK, N], BF16, name="x_raw%d" % b) for b in range(B)]
+        qb_bf = const.tile([P, HEADS, PACK], BF16, name="qb_bf")
+        kb_bf = const.tile([P, HEADS, PACK], BF16, name="kb_bf")
 
         def load_w(m):
             nc.sync.dma_start(
@@ -37,162 +40,275 @@ def tile_acd_pa_t_kernel(tc, x, q_w, q_b, k_w, k_b, out_0, out_1, out_2):
                 in_=w_dram[m].rearrange("(p t) c -> p (t c)", t=PACK),
             )
 
-        def load_x(bp):
+        def load_x(b):
             nc.sync.dma_start(
-                out=x_raw[bp][:].rearrange("p b j n -> p b (j n)"),
-                in_=x[2 * bp : 2 * bp + 2].rearrange("b (p j) h w -> p b (j h w)", j=PACK),
+                out=x_raw[b][:].rearrange("p j n -> p (j n)"),
+                in_=x[b].rearrange("(p j) h w -> p (j h w)", j=PACK),
             )
 
-        qb_bf = const.tile([P, HEADS, PACK], BF16, name="qb_bf")
-        kb_bf = const.tile([P, HEADS, PACK], BF16, name="kb_bf")
+        with nc.allow_non_contiguous_dma(reason="bias: four neighbouring values to a partition"):
+            nc.scalar.dma_start(out=qb_bf[:], in_=q_b.rearrange("h (p t) -> p h t", t=PACK))
+            nc.scalar.dma_start(out=kb_bf[:], in_=k_b.rearrange("h (p t) -> p h t", t=PACK))
         load_w(0)
         load_x(0)
         load_w(1)
-        with nc.allow_non_contiguous_dma(reason="bias: four neighbouring values to a partition"):
-            nc.sync.dma_start(out=qb_bf[:], in_=q_b.rearrange("h (p t) -> p h t", t=PACK))
-            nc.sync.dma_start(out=kb_bf[:], in_=k_b.rearrange("h (p t) -> p h t", t=PACK))
+        load_x(1)
         load_w(2)
         load_w(3)
-        for bp in range(1, B // 2):
-            load_x(bp)
+        for b in range(2, B):
+            load_x(b)
 
         ident = const.tile([P, P], F32, name="ident")
         make_identity(nc, ident[:])
-        ones_pos = const.tile([P, P], F32, name="ones_pos")
-        ones_neg = const.tile([P, P], F32, name="ones_neg")
-        nc.vector.memset(ones_pos[:], 1.0)
-        nc.vector.memset(ones_neg[:], -1.0)
+        ones = const.tile([P, P], F32, name="ones")
+        nc.vector.memset(ones[:], 1.0)
         warm_in = const.tile([P, 1], F32, name="warm_in")
         warm_out = const.tile([P, 1], F32, name="warm_out")
         nc.vector.memset(warm_in[:], 0.0)
         nc.scalar.activation(out=warm_out[:], in_=warm_in[:], func=ACT.Sigmoid)
+        junk = const.tile([P, 1], F32, name="junk")
         bias_f = const.tile([P, HEADS, 2, PACK], F32, name="bias_f")
-        nc.vector.tensor_copy(out=bias_f[:, :, 0, :], in_=qb_bf[:])
-        nc.vector.tensor_copy(out=bias_f[:, :, 1, :], in_=kb_bf[:])
 
         w_codes = [const.tile([P, HD], U32, name="w_codes%d" % m, align_bytes=64) for m in range(4)]
         w_scales = [const.tile([P, HD], U8, name="w_scales%d" % m, align_bytes=64) for m in range(4)]
+        w_banks = {}
+        w_grouped = {}
 
-        def prepare_w(m):
+        def w_transpose(m):
             words = w_raw[m][:].bitcast(F32)
-            w_grouped = work.tile([P, PACK, P, PACK], BF16, name="w_grouped", align_bytes=64)
-            grouped_words = w_grouped[:].bitcast(F32)
+            tags = ("sim", "sim") if m % 2 == 0 else ("dsum", "diff")
             for half in range(2):
-                bank = psum.tile([P, 2, 2, P], F32, name="w_bank", tag="qk", bufs=4)
+                bank = psum.tile([P, 2, 2, P], F32, name="w_bank", tag=tags[half], bufs=(2 if m % 2 == 0 else 1))
                 for tt in range(2):
                     for u in range(2):
                         nc.tensor.transpose(bank[:, tt, u, :], words[:, 2 * half + tt, u : C // 2 : 2], ident[:])
+                w_banks[(m, half)] = bank
+
+        def w_empty(m, on_vector):
+            grouped = work.tile([P, PACK, P, PACK], BF16, name="w_grouped", align_bytes=64)
+            w_grouped[m] = grouped
+            grouped_words = grouped[:].bitcast(F32)
+            for half in range(2):
                 dst = grouped_words[:, 2 * half : 2 * half + 2, :, :]
-                src = bank[:].rearrange("p t u d -> p t d u")
-                if half == 0:
+                src = w_banks[(m, half)][:].rearrange("p t u d -> p t d u")
+                if on_vector:
                     nc.vector.tensor_copy(out=dst, in_=src)
                 else:
                     nc.scalar.copy(out=dst, in_=src)
-            nc.vector.quantize_mx(
-                out=w_codes[m][:].bitcast(FP8X4),
-                scales=w_scales[m][:],
-                in_=w_grouped[:].rearrange("p t d j -> p (t d j)"),
+
+        def w_quantise(m):
+            flat = w_grouped[m][:].rearrange("p t d j -> p (t d j)")
+            if m == 3:
+                nc.vector.tensor_scalar_mul(out=flat, in0=flat, scalar1=-1.0)
+            nc.vector.quantize_mx(out=w_codes[m][:].bitcast(FP8X4), scales=w_scales[m][:], in_=flat)
+
+        x_grouped = {}
+        x_codes = {}
+        x_scales = {}
+
+        def x_regroup(b):
+            grouped = work.tile([P, N, PACK], BF16, name="x_grouped", align_bytes=64)
+            x_grouped[b] = grouped
+            nc.scalar.copy(
+                out=grouped[:].rearrange("p (c i) t -> p c t i", i=4),
+                in_=x_raw[b][:].rearrange("p t (c i) -> p c t i", i=4),
             )
 
-        def prepare_x(bp):
-            x_grouped = work.tile([P, 2, N, PACK], BF16, name="x_grouped", align_bytes=64)
-            for b2 in range(2):
-                nc.scalar.copy(
-                    out=x_grouped[:, b2].rearrange("p (c i) t -> p c t i", i=4),
-                    in_=x_raw[bp][:, b2].rearrange("p t (c i) -> p c t i", i=4),
-                )
-            x_codes = work.tile([P, 2 * N], U32, name="x_codes", align_bytes=64)
-            x_scales = work.tile([P, 2 * N], U8, name="x_scales", align_bytes=64)
+        def x_quantise(b):
+            x_codes[b] = work.tile([P, N], U32, name="x_codes", bufs=4, align_bytes=64)
+            x_scales[b] = work.tile([P, N], U8, name="x_scales", bufs=4, align_bytes=64)
             nc.vector.quantize_mx(
-                out=x_codes[:].bitcast(FP8X4),
-                scales=x_scales[:],
-                in_=x_grouped[:].rearrange("p b n j -> p (b n j)"),
+                out=x_codes[b][:].bitcast(FP8X4),
+                scales=x_scales[b][:],
+                in_=x_grouped[b][:].rearrange("p n j -> p (n j)"),
             )
-            return x_codes, x_scales
 
-        prepare_w(0)
-        xq = prepare_x(0)
-        prepare_w(1)
-        prepare_w(2)
-        prepare_w(3)
+        banks = {}
+        qk_grouped = {}
+        qk_codes = {}
+        qk_scales = {}
+        sim_banks = {}
+        dsum_banks = {}
+        dsum_sb = {}
+        diff_banks = {}
+        sim_sb = {}
+        att = {}
+        enhanced = {}
 
-        for bp in range(B // 2):
-            x_codes, x_scales = xq
-            for b2 in range(2):
-                b = 2 * bp + b2
-                sim_sb = work.tile([P, HEADS, 2, N], F32, name="sim_sb", bufs=3)
-                for h in range(HEADS):
-                    qk_grouped = work.tile([P, 2, N, PACK], BF16, name="qk_grouped", bufs=4, align_bytes=64)
-                    for qk in range(2):
-                        m = 2 * h + qk
-                        for nh in range(2):
-                            bank = psum.tile([P, PACK, P], F32, name="qk_bank", tag="qk", bufs=4)
-                            cols = slice(b2 * N + nh * P, b2 * N + (nh + 1) * P)
-                            for t in range(PACK):
-                                nc.tensor.matmul_mx(
-                                    out=bank[:, t, :],
-                                    lhsT=w_codes[m][:, t * P : (t + 1) * P].bitcast(FP8X4),
-                                    lhsT_scale=w_scales[m][:, t * P : (t + 1) * P],
-                                    rhs=x_codes[:, cols].bitcast(FP8X4),
-                                    rhs_scale=x_scales[:, cols],
-                                    start=True,
-                                    stop=True,
-                                )
-                            nc.vector.tensor_tensor(
-                                out=qk_grouped[:, qk, nh * P : (nh + 1) * P, :],
-                                in0=bank[:].rearrange("p t c -> p c t"),
-                                in1=bias_f[:, h, qk, :].unsqueeze(1).to_broadcast([P, P, PACK]),
-                                op=ALU.add,
-                            )
-                    qk_codes = work.tile([P, 2 * N], U32, name="qk_codes", bufs=3, align_bytes=64)
-                    qk_scales = work.tile([P, 2 * N], U8, name="qk_scales", bufs=3, align_bytes=64)
-                    nc.vector.quantize_mx(
-                        out=qk_codes[:].bitcast(FP8X4),
-                        scales=qk_scales[:],
-                        in_=qk_grouped[:].rearrange("p a n j -> p (a n j)"),
-                    )
-                    sim_bank = psum.tile([P, 2, N], F32, name="sim_bank", tag="sim", bufs=2)
-                    for qt in range(2):
-                        nc.tensor.matmul_mx(
-                            out=sim_bank[:, qt, :],
-                            lhsT=qk_codes[:, qt * P : (qt + 1) * P].bitcast(FP8X4),
-                            lhsT_scale=qk_scales[:, qt * P : (qt + 1) * P],
-                            rhs=qk_codes[:, N : 2 * N].bitcast(FP8X4),
-                            rhs_scale=qk_scales[:, N : 2 * N],
-                            start=True,
-                            stop=True,
-                        )
-                    nc.scalar.activation(out=sim_sb[:, h], in_=sim_bank[:], func=ACT.Copy, scale=inv_sqrt)
-                nc.sync.dma_start(
-                    out=out_2[b].rearrange("h (qt p) k -> p (h qt) k", p=P),
-                    in_=sim_sb[:].rearrange("p h qt k -> p (h qt) k"),
+        def fill(b, i):
+            m, nh = i // 2, i % 2
+            bank = psum.tile([P, PACK, P], F32, name="qk_bank", tag="qk", bufs=4)
+            banks[(b, i)] = bank
+            cols = slice(nh * P, (nh + 1) * P)
+            for t in range(PACK):
+                nc.tensor.matmul_mx(
+                    out=bank[:, t, :],
+                    lhsT=w_codes[m][:, t * P : (t + 1) * P].bitcast(FP8X4),
+                    lhsT_scale=w_scales[m][:, t * P : (t + 1) * P],
+                    rhs=x_codes[b][:, cols].bitcast(FP8X4),
+                    rhs_scale=x_scales[b][:, cols],
+                    start=True,
+                    stop=True,
                 )
-                diff = psum.tile([P, N], F32, name="diff", tag="diff", bufs=2)
-                for h in range(HEADS):
-                    for qt in range(2):
-                        nc.tensor.matmul(
-                            out=diff[:],
-                            lhsT=(ones_pos if h == 0 else ones_neg)[:],
-                            rhs=sim_sb[:, h, qt, :],
-                            start=(h == 0 and qt == 0),
-                            stop=(h == 1 and qt == 1),
-                        )
-                att = work.tile([P, HEADS, N], F32, name="att", bufs=3)
-                nc.scalar.activation(out=att[:, 0, :], in_=diff[:], func=ACT.Sigmoid)
-                nc.scalar.activation(out=att[:, 1, :], in_=diff[:], func=ACT.Sigmoid, scale=-1.0)
-                nc.sync.dma_start(out=out_0[b : b + 1].rearrange("o h i j -> o h (i j)"), in_=att[0:1, :, :])
-                enhanced = work.tile([P, HEADS, PACK, N], F32, name="enhanced", bufs=4)
-                for h in range(HEADS):
-                    engine = nc.vector if (b, h) in VECTOR_PRODUCTS else nc.gpsimd
-                    engine.tensor_tensor(
-                        out=enhanced[:, h],
-                        in0=x_raw[bp][:, b2],
-                        in1=att[:, h, :].unsqueeze(1).to_broadcast([P, PACK, N]),
-                        op=ALU.mult,
-                    )
-                nc.sync.dma_start(
-                    out=out_1[b].rearrange("(h p j) i w -> p h (j i w)", h=HEADS, j=PACK),
-                    in_=enhanced[:].rearrange("p h j n -> p h (j n)"),
+
+        def empty(b, i):
+            m, nh = i // 2, i % 2
+            if i == 0:
+                qk_grouped[b] = work.tile([P, 4, N, PACK], BF16, name="qk_grouped", align_bytes=64)
+            nc.vector.tensor_tensor(
+                out=qk_grouped[b][:, m, nh * P : (nh + 1) * P, :],
+                in0=banks[(b, i)][:].rearrange("p t c -> p c t"),
+                in1=bias_f[:, m // 2, m % 2, :].unsqueeze(1).to_broadcast([P, P, PACK]),
+                op=ALU.add,
+            )
+
+        def qk_quantise(b):
+            qk_codes[b] = work.tile([P, 4 * N], U32, name="qk_codes", align_bytes=64)
+            qk_scales[b] = work.tile([P, 4 * N], U8, name="qk_scales", align_bytes=64)
+            nc.vector.quantize_mx(
+                out=qk_codes[b][:].bitcast(FP8X4),
+                scales=qk_scales[b][:],
+                in_=qk_grouped[b][:].rearrange("p m n j -> p (m n j)"),
+            )
+
+        def sim_pass(b, h, qt, out, start, stop):
+            q0 = 2 * h * N + qt * P
+            k0 = (2 * h + 1) * N
+            nc.tensor.matmul_mx(
+                out=out,
+                lhsT=qk_codes[b][:, q0 : q0 + P].bitcast(FP8X4),
+                lhsT_scale=qk_scales[b][:, q0 : q0 + P],
+                rhs=qk_codes[b][:, k0 : k0 + N].bitcast(FP8X4),
+                rhs_scale=qk_scales[b][:, k0 : k0 + N],
+                start=start,
+                stop=stop,
+            )
+
+        def stage2(b):
+            dsum = psum.tile([P, N], F32, name="dsum", tag="dsum", bufs=1)
+            dsum_banks[b] = dsum
+            for h in range(HEADS):
+                for qt in range(2):
+                    sim_pass(b, h, qt, dsum[:], h == 0 and qt == 0, h == 1 and qt == 1)
+            for h in range(HEADS):
+                bank = psum.tile([P, 2, N], F32, name="sim_bank", tag="sim", bufs=2)
+                sim_banks[(b, h)] = bank
+                for qt in range(2):
+                    sim_pass(b, h, qt, bank[:, qt, :], True, True)
+            dsum_sb[b] = work.tile([P, N], F32, name="dsum_sb")
+            nc.scalar.copy(out=dsum_sb[b][:], in_=dsum[:])
+            sim_sb[b] = work.tile([P, HEADS, 2, N], F32, name="sim_sb", bufs=3)
+            for h in range(HEADS):
+                nc.scalar.activation(
+                    out=sim_sb[b][:, h],
+                    in_=sim_banks[(b, h)][:],
+                    func=ACT.Copy,
+                    scale=(inv_sqrt if h == 0 else -inv_sqrt),
                 )
-                if b2 == 0 and bp + 1 < B // 2:
-                    xq = prepare_x(bp + 1)
+            nc.sync.dma_start(
+                out=out_2[b].rearrange("h (qt p) k -> p (h qt) k", p=P),
+                in_=sim_sb[b][:].rearrange("p h qt k -> p (h qt) k"),
+            )
+
+        def gates(b):
+            diff = psum.tile([P, N], F32, name="diff", tag="diff", bufs=1)
+            nc.tensor.matmul(out=diff[:], lhsT=ones[:], rhs=dsum_sb[b][:], start=True, stop=True)
+            att[b] = work.tile([P, HEADS, N], F32, name="att", bufs=3)
+            nc.scalar.activation(out=att[b][:, 0, :], in_=diff[:], func=ACT.Sigmoid, scale=inv_sqrt)
+            nc.scalar.activation(out=att[b][:, 1, :], in_=diff[:], func=ACT.Sigmoid, scale=-inv_sqrt)
+            nc.sync.dma_start(out=out_0[b : b + 1].rearrange("o h i j -> o h (i j)"), in_=att[b][0:1, :, :])
+
+        def product_gpsimd(b, after):
+            nc.gpsimd.tensor_copy(out=junk[:], in_=qk_codes[after][:, 0:1].bitcast(F32))
+            enhanced[b] = work.tile([P, HEADS, PACK, N], F32, name="enhanced", bufs=3)
+            nc.gpsimd.tensor_tensor(
+                out=enhanced[b][:],
+                in0=x_raw[b][:].unsqueeze(1).to_broadcast([P, HEADS, PACK, N]),
+                in1=att[b][:].unsqueeze(2).to_broadcast([P, HEADS, PACK, N]),
+                op=ALU.mult,
+            )
+
+        def store_enhanced(b):
+            nc.sync.dma_start(
+                out=out_1[b].rearrange("(h p j) i w -> p h (j i w)", h=HEADS, j=PACK),
+                in_=enhanced[b][:].rearrange("p h j n -> p h (j n)"),
+            )
+
+        def product_vector(b):
+            enhanced[b] = work.tile([P, HEADS, PACK, N], F32, name="enhanced", bufs=3)
+            for h in range(HEADS):
+                nc.vector.tensor_tensor(
+                    out=enhanced[b][:, h],
+                    in0=x_raw[b][:],
+                    in1=att[b][:, h, :].unsqueeze(1).to_broadcast([P, PACK, N]),
+                    op=ALU.mult,
+                )
+                nc.sync.dma_start(
+                    out=out_1[b, h * C : (h + 1) * C].rearrange("(p j) i w -> p (j i w)", j=PACK),
+                    in_=enhanced[b][:, h].rearrange("p j n -> p (j n)"),
+                )
+
+        w_transpose(0)
+        w_empty(0, True)
+        x_regroup(0)
+        x_regroup(1)
+        w_quantise(0)
+        x_quantise(0)
+        w_transpose(1)
+        w_empty(1, False)
+        fill(0, 0)
+        fill(0, 1)
+        w_transpose(2)
+        w_empty(2, False)
+        nc.vector.tensor_copy(out=bias_f[:, :, 0, :], in_=qb_bf[:])
+        nc.vector.tensor_copy(out=bias_f[:, 0, 1, :], in_=kb_bf[:, 0, :])
+        nc.vector.tensor_scalar_mul(out=bias_f[:, 1, 1, :], in0=kb_bf[:, 1, :], scalar1=-1.0)
+        empty(0, 0)
+        w_quantise(1)
+        fill(0, 2)
+        fill(0, 3)
+        w_transpose(3)
+        w_empty(3, False)
+        x_regroup(2)
+        empty(0, 1)
+        x_quantise(1)
+        empty(0, 2)
+        empty(0, 3)
+        w_quantise(2)
+        fill(0, 4)
+        fill(0, 5)
+        w_quantise(3)
+        fill(0, 6)
+        fill(0, 7)
+
+        for s in range(B + 2):
+            if s >= 2 and (s - 2) in VECTOR_BATCHES:
+                product_vector(s - 2)
+            if 1 <= s <= B:
+                stage2(s - 1)
+            if s >= 2 and (s - 2) not in VECTOR_BATCHES:
+                product_gpsimd(s - 2, s - 1)
+            if 1 <= s < B:
+                empty(s, 0)
+                empty(s, 1)
+                fill(s, 4)
+                fill(s, 5)
+            if 1 <= s <= B:
+                gates(s - 1)
+            if s >= 2 and (s - 2) not in VECTOR_BATCHES:
+                store_enhanced(s - 2)
+            if 1 <= s < B:
+                if s + 2 < B:
+                    x_regroup(s + 2)
+                empty(s, 2)
+                empty(s, 3)
+                fill(s, 6)
+                fill(s, 7)
+            if s < B:
+                for i in range(4, 8):
+                    empty(s, i)
+                    if s + 1 < B:
+                        fill(s + 1, i - 4)
+                if s + 2 < B:
+                    x_quantise(s + 2)
+                qk_quantise(s)

@@ -17,6 +17,8 @@ B, C, N, HEADS, HD = 16, 512, 256, 2, 512
 PACK = 4
 FLOPS = 2 * B * HEADS * 2 * N * C * HD + 2 * B * HEADS * N * N * HD
 VECTOR_BATCHES = (14, 15)
+GPSIMD_PLANES = 3
+SCALAR_MATRIX = 3
 
 
 def tile_acd_pa_t_kernel(tc, x, q_w, q_b, k_w, k_b, out_0, out_1, out_2):
@@ -76,9 +78,8 @@ def tile_acd_pa_t_kernel(tc, x, q_w, q_b, k_w, k_b, out_0, out_1, out_2):
 
         def w_transpose(m):
             words = w_raw[m][:].bitcast(F32)
-            tags = ("sim", "sim") if m % 2 == 0 else ("dsum", "diff")
             for half in range(2):
-                bank = psum.tile([P, 2, 2, P], F32, name="w_bank", tag=tags[half], bufs=(2 if m % 2 == 0 else 1))
+                bank = psum.tile([P, 2, 2, P], F32, name="w_bank", tag=("sim" if m % 2 == 0 else "sq"), bufs=2)
                 for tt in range(2):
                     for u in range(2):
                         nc.tensor.transpose(bank[:, tt, u, :], words[:, 2 * half + tt, u : C // 2 : 2], ident[:])
@@ -107,7 +108,7 @@ def tile_acd_pa_t_kernel(tc, x, q_w, q_b, k_w, k_b, out_0, out_1, out_2):
         x_scales = {}
 
         def x_regroup(b):
-            grouped = work.tile([P, N, PACK], BF16, name="x_grouped", align_bytes=64)
+            grouped = work.tile([P, N, PACK], BF16, name="x_grouped", bufs=3, align_bytes=64)
             x_grouped[b] = grouped
             nc.scalar.copy(
                 out=grouped[:].rearrange("p (c i) t -> p c t i", i=4),
@@ -128,16 +129,17 @@ def tile_acd_pa_t_kernel(tc, x, q_w, q_b, k_w, k_b, out_0, out_1, out_2):
         qk_codes = {}
         qk_scales = {}
         sim_banks = {}
-        dsum_banks = {}
         dsum_sb = {}
-        diff_banks = {}
+        dd_banks = {}
+        order = [(b, i) for b in range(B) for i in range(8 if b == 0 else 6)]
+        state = {"next": 0}
         sim_sb = {}
         att = {}
         enhanced = {}
 
         def fill(b, i):
             m, nh = i // 2, i % 2
-            bank = psum.tile([P, PACK, P], F32, name="qk_bank", tag="qk", bufs=4)
+            bank = psum.tile([P, PACK, P], F32, name="qk_bank", tag="qk", bufs=3)
             banks[(b, i)] = bank
             cols = slice(nh * P, (nh + 1) * P)
             for t in range(PACK):
@@ -151,10 +153,51 @@ def tile_acd_pa_t_kernel(tc, x, q_w, q_b, k_w, k_b, out_0, out_1, out_2):
                     stop=True,
                 )
 
+        def fill_next():
+            k = state["next"]
+            if k < len(order):
+                fill(order[k][0], order[k][1])
+            state["next"] = k + 1
+
+        def grouped_of(b):
+            if b not in qk_grouped:
+                qk_grouped[b] = work.tile([P, 4, N, PACK], BF16, name="qk_grouped", align_bytes=64)
+            return qk_grouped[b]
+
+        def scalar_path(b):
+            m = SCALAR_MATRIX
+            planes = work.tile([P, PACK, N], BF16, name="planes")
+            sq = []
+            for th in range(2):
+                bank = psum.tile([P, 2, N], F32, name="sq_bank", tag="sq", bufs=2)
+                sq.append(bank)
+                for tt in range(2):
+                    t = 2 * th + tt
+                    nc.tensor.matmul_mx(
+                        out=bank[:, tt, :],
+                        lhsT=w_codes[m][:, t * P : (t + 1) * P].bitcast(FP8X4),
+                        lhsT_scale=w_scales[m][:, t * P : (t + 1) * P],
+                        rhs=x_codes[b][:].bitcast(FP8X4),
+                        rhs_scale=x_scales[b][:],
+                        start=True,
+                        stop=True,
+                    )
+            for t in range(PACK):
+                nc.scalar.activation(
+                    out=planes[:, t, :],
+                    in_=sq[t // 2][:, t % 2, :],
+                    func=ACT.Identity,
+                    bias=bias_f[:, m // 2, m % 2, t : t + 1],
+                    scale=1.0,
+                )
+            nc.scalar.copy(
+                out=grouped_of(b)[:, m].rearrange("p (c i) t -> p c t i", i=4),
+                in_=planes[:].rearrange("p t (c i) -> p c t i", i=4),
+            )
+
         def empty(b, i):
             m, nh = i // 2, i % 2
-            if i == 0:
-                qk_grouped[b] = work.tile([P, 4, N, PACK], BF16, name="qk_grouped", align_bytes=64)
+            grouped_of(b)
             nc.vector.tensor_tensor(
                 out=qk_grouped[b][:, m, nh * P : (nh + 1) * P, :],
                 in0=banks[(b, i)][:].rearrange("p t c -> p c t"),
@@ -184,47 +227,55 @@ def tile_acd_pa_t_kernel(tc, x, q_w, q_b, k_w, k_b, out_0, out_1, out_2):
                 stop=stop,
             )
 
-        def stage2(b):
-            dsum = psum.tile([P, N], F32, name="dsum", tag="dsum", bufs=1)
-            dsum_banks[b] = dsum
+        def stage2_sum(b):
+            dd = psum.tile([P, 2, N], F32, name="dd", tag="dd", bufs=1)
+            dd_banks[b] = dd
             for h in range(HEADS):
                 for qt in range(2):
-                    sim_pass(b, h, qt, dsum[:], h == 0 and qt == 0, h == 1 and qt == 1)
-            for h in range(HEADS):
-                bank = psum.tile([P, 2, N], F32, name="sim_bank", tag="sim", bufs=2)
-                sim_banks[(b, h)] = bank
-                for qt in range(2):
-                    sim_pass(b, h, qt, bank[:, qt, :], True, True)
+                    sim_pass(b, h, qt, dd[:, 0, :], h == 0 and qt == 0, h == 1 and qt == 1)
             dsum_sb[b] = work.tile([P, N], F32, name="dsum_sb")
-            nc.scalar.copy(out=dsum_sb[b][:], in_=dsum[:])
-            sim_sb[b] = work.tile([P, HEADS, 2, N], F32, name="sim_sb", bufs=3)
-            for h in range(HEADS):
-                nc.scalar.activation(
-                    out=sim_sb[b][:, h],
-                    in_=sim_banks[(b, h)][:],
-                    func=ACT.Copy,
-                    scale=(inv_sqrt if h == 0 else -inv_sqrt),
-                )
-            nc.sync.dma_start(
-                out=out_2[b].rearrange("h (qt p) k -> p (h qt) k", p=P),
-                in_=sim_sb[b][:].rearrange("p h qt k -> p (h qt) k"),
+            nc.scalar.copy(out=dsum_sb[b][:], in_=dd[:, 0, :])
+
+        def stage2_sim(b, h):
+            bank = psum.tile([P, 2, N], F32, name="sim_bank", tag="sim", bufs=2)
+            for qt in range(2):
+                sim_pass(b, h, qt, bank[:, qt, :], True, True)
+            if h == 0:
+                sim_sb[b] = work.tile([P, HEADS, 2, N], F32, name="sim_sb", bufs=3)
+            nc.scalar.activation(
+                out=sim_sb[b][:, h], in_=bank[:], func=ACT.Copy, scale=(inv_sqrt if h == 0 else -inv_sqrt)
             )
+            if h == 1:
+                nc.sync.dma_start(
+                    out=out_2[b].rearrange("h (qt p) k -> p (h qt) k", p=P),
+                    in_=sim_sb[b][:].rearrange("p h qt k -> p (h qt) k"),
+                )
 
         def gates(b):
-            diff = psum.tile([P, N], F32, name="diff", tag="diff", bufs=1)
-            nc.tensor.matmul(out=diff[:], lhsT=ones[:], rhs=dsum_sb[b][:], start=True, stop=True)
+            diff = dd_banks[b][:, 1, :]
+            nc.tensor.matmul(out=diff, lhsT=ones[:], rhs=dsum_sb[b][:], start=True, stop=True)
             att[b] = work.tile([P, HEADS, N], F32, name="att", bufs=3)
-            nc.scalar.activation(out=att[b][:, 0, :], in_=diff[:], func=ACT.Sigmoid, scale=inv_sqrt)
-            nc.scalar.activation(out=att[b][:, 1, :], in_=diff[:], func=ACT.Sigmoid, scale=-inv_sqrt)
+            nc.scalar.activation(out=att[b][:, 0, :], in_=diff, func=ACT.Sigmoid, scale=inv_sqrt)
+            nc.scalar.activation(out=att[b][:, 1, :], in_=diff, func=ACT.Sigmoid, scale=-inv_sqrt)
             nc.sync.dma_start(out=out_0[b : b + 1].rearrange("o h i j -> o h (i j)"), in_=att[b][0:1, :, :])
 
         def product_gpsimd(b, after):
             nc.gpsimd.tensor_copy(out=junk[:], in_=qk_codes[after][:, 0:1].bitcast(F32))
             enhanced[b] = work.tile([P, HEADS, PACK, N], F32, name="enhanced", bufs=3)
+            g = GPSIMD_PLANES
             nc.gpsimd.tensor_tensor(
-                out=enhanced[b][:],
-                in0=x_raw[b][:].unsqueeze(1).to_broadcast([P, HEADS, PACK, N]),
-                in1=att[b][:].unsqueeze(2).to_broadcast([P, HEADS, PACK, N]),
+                out=enhanced[b][:, :, 0:g, :],
+                in0=x_raw[b][:, 0:g, :].unsqueeze(1).to_broadcast([P, HEADS, g, N]),
+                in1=att[b][:].unsqueeze(2).to_broadcast([P, HEADS, g, N]),
+                op=ALU.mult,
+            )
+
+        def product_rest(b):
+            g = GPSIMD_PLANES
+            nc.vector.tensor_tensor(
+                out=enhanced[b][:, :, g:PACK, :],
+                in0=x_raw[b][:, g:PACK, :].unsqueeze(1).to_broadcast([P, HEADS, PACK - g, N]),
+                in1=att[b][:].unsqueeze(2).to_broadcast([P, HEADS, PACK - g, N]),
                 op=ALU.mult,
             )
 
@@ -256,8 +307,8 @@ def tile_acd_pa_t_kernel(tc, x, q_w, q_b, k_w, k_b, out_0, out_1, out_2):
         x_quantise(0)
         w_transpose(1)
         w_empty(1, False)
-        fill(0, 0)
-        fill(0, 1)
+        fill_next()
+        fill_next()
         w_transpose(2)
         w_empty(2, False)
         nc.vector.tensor_copy(out=bias_f[:, :, 0, :], in_=qb_bf[:])
@@ -265,50 +316,56 @@ def tile_acd_pa_t_kernel(tc, x, q_w, q_b, k_w, k_b, out_0, out_1, out_2):
         nc.vector.tensor_scalar_mul(out=bias_f[:, 1, 1, :], in0=kb_bf[:, 1, :], scalar1=-1.0)
         empty(0, 0)
         w_quantise(1)
-        fill(0, 2)
-        fill(0, 3)
+        fill_next()
+        fill_next()
         w_transpose(3)
         w_empty(3, False)
         x_regroup(2)
         empty(0, 1)
         x_quantise(1)
         empty(0, 2)
-        empty(0, 3)
         w_quantise(2)
-        fill(0, 4)
-        fill(0, 5)
+        fill_next()
+        fill_next()
+        empty(0, 3)
         w_quantise(3)
-        fill(0, 6)
-        fill(0, 7)
+        fill_next()
+        empty(0, 4)
+        fill_next()
+        scalar_path(1)
+        x_regroup(3)
+        for i in range(5, 8):
+            empty(0, i)
+            fill_next()
+        x_quantise(2)
+        qk_quantise(0)
 
-        for s in range(B + 2):
+        for s in range(1, B + 2):
             if s >= 2 and (s - 2) in VECTOR_BATCHES:
                 product_vector(s - 2)
-            if 1 <= s <= B:
-                stage2(s - 1)
             if s >= 2 and (s - 2) not in VECTOR_BATCHES:
                 product_gpsimd(s - 2, s - 1)
-            if 1 <= s < B:
-                empty(s, 0)
-                empty(s, 1)
-                fill(s, 4)
-                fill(s, 5)
-            if 1 <= s <= B:
-                gates(s - 1)
+            for idx in range(6):
+                if s <= B:
+                    if idx == 0:
+                        stage2_sum(s - 1)
+                    if idx == 1:
+                        stage2_sim(s - 1, 0)
+                    if idx == 2:
+                        stage2_sim(s - 1, 1)
+                    if idx == 3:
+                        gates(s - 1)
+                        if s + 1 < B:
+                            scalar_path(s + 1)
+                        if s + 3 < B:
+                            x_regroup(s + 3)
+                if s < B:
+                    empty(s, idx)
+                    fill_next()
             if s >= 2 and (s - 2) not in VECTOR_BATCHES:
+                product_rest(s - 2)
                 store_enhanced(s - 2)
-            if 1 <= s < B:
-                if s + 2 < B:
-                    x_regroup(s + 2)
-                empty(s, 2)
-                empty(s, 3)
-                fill(s, 6)
-                fill(s, 7)
             if s < B:
-                for i in range(4, 8):
-                    empty(s, i)
-                    if s + 1 < B:
-                        fill(s + 1, i - 4)
                 if s + 2 < B:
                     x_quantise(s + 2)
                 qk_quantise(s)

@@ -17,7 +17,7 @@ B, C, N, HEADS, HD = 16, 512, 256, 2, 512
 PACK = 4
 FLOPS = 2 * B * HEADS * 2 * N * C * HD + 2 * B * HEADS * N * N * HD
 VECTOR_BATCHES = (14, 15)
-GPSIMD_PLANES = 3
+GPSIMD_COLUMNS = 176
 SCALAR_MATRIX = 3
 
 
@@ -68,7 +68,6 @@ def tile_acd_pa_t_kernel(tc, x, q_w, q_b, k_w, k_b, out_0, out_1, out_2):
         warm_out = const.tile([P, 1], F32, name="warm_out")
         nc.vector.memset(warm_in[:], 0.0)
         nc.scalar.activation(out=warm_out[:], in_=warm_in[:], func=ACT.Sigmoid)
-        junk = const.tile([P, 1], F32, name="junk")
         bias_f = const.tile([P, HEADS, 2, PACK], F32, name="bias_f")
 
         w_codes = [const.tile([P, HD], U32, name="w_codes%d" % m, align_bytes=64) for m in range(4)]
@@ -161,7 +160,7 @@ def tile_acd_pa_t_kernel(tc, x, q_w, q_b, k_w, k_b, out_0, out_1, out_2):
 
         def grouped_of(b):
             if b not in qk_grouped:
-                qk_grouped[b] = work.tile([P, 4, N, PACK], BF16, name="qk_grouped", align_bytes=64)
+                qk_grouped[b] = work.tile([P, 4, N, PACK], BF16, name="qk_grouped", tag="big%d" % (b % 3), bufs=1, align_bytes=64)
             return qk_grouped[b]
 
         def scalar_path(b):
@@ -259,23 +258,14 @@ def tile_acd_pa_t_kernel(tc, x, q_w, q_b, k_w, k_b, out_0, out_1, out_2):
             nc.scalar.activation(out=att[b][:, 1, :], in_=diff, func=ACT.Sigmoid, scale=-inv_sqrt)
             nc.sync.dma_start(out=out_0[b : b + 1].rearrange("o h i j -> o h (i j)"), in_=att[b][0:1, :, :])
 
-        def product_gpsimd(b, after):
-            nc.gpsimd.tensor_copy(out=junk[:], in_=qk_codes[after][:, 0:1].bitcast(F32))
-            enhanced[b] = work.tile([P, HEADS, PACK, N], F32, name="enhanced", bufs=3)
-            g = GPSIMD_PLANES
-            nc.gpsimd.tensor_tensor(
-                out=enhanced[b][:, :, 0:g, :],
-                in0=x_raw[b][:, 0:g, :].unsqueeze(1).to_broadcast([P, HEADS, g, N]),
-                in1=att[b][:].unsqueeze(2).to_broadcast([P, HEADS, g, N]),
-                op=ALU.mult,
-            )
+        def enhanced_tile(b):
+            enhanced[b] = work.tile([P, HEADS, PACK, N], F32, name="enhanced", tag="big%d" % ((b + 1) % 3), bufs=1, align_bytes=64)
 
-        def product_rest(b):
-            g = GPSIMD_PLANES
-            nc.vector.tensor_tensor(
-                out=enhanced[b][:, :, g:PACK, :],
-                in0=x_raw[b][:, g:PACK, :].unsqueeze(1).to_broadcast([P, HEADS, PACK - g, N]),
-                in1=att[b][:].unsqueeze(2).to_broadcast([P, HEADS, PACK - g, N]),
+        def product(engine, b, lo, hi):
+            engine.tensor_tensor(
+                out=enhanced[b][:, :, :, lo:hi],
+                in0=x_raw[b][:, :, lo:hi].unsqueeze(1).to_broadcast([P, HEADS, PACK, hi - lo]),
+                in1=att[b][:, :, lo:hi].unsqueeze(2).to_broadcast([P, HEADS, PACK, hi - lo]),
                 op=ALU.mult,
             )
 
@@ -286,7 +276,7 @@ def tile_acd_pa_t_kernel(tc, x, q_w, q_b, k_w, k_b, out_0, out_1, out_2):
             )
 
         def product_vector(b):
-            enhanced[b] = work.tile([P, HEADS, PACK, N], F32, name="enhanced", bufs=3)
+            enhanced_tile(b)
             for h in range(HEADS):
                 nc.vector.tensor_tensor(
                     out=enhanced[b][:, h],
@@ -344,11 +334,14 @@ def tile_acd_pa_t_kernel(tc, x, q_w, q_b, k_w, k_b, out_0, out_1, out_2):
             if s >= 2 and (s - 2) in VECTOR_BATCHES:
                 product_vector(s - 2)
             if s >= 2 and (s - 2) not in VECTOR_BATCHES:
-                product_gpsimd(s - 2, s - 1)
+                enhanced_tile(s - 2)
+                product(nc.gpsimd, s - 2, 0, GPSIMD_COLUMNS)
             for idx in range(6):
                 if s <= B:
                     if idx == 0:
                         stage2_sum(s - 1)
+                        if s + 3 < B:
+                            x_regroup(s + 3)
                     if idx == 1:
                         stage2_sim(s - 1, 0)
                     if idx == 2:
@@ -357,13 +350,11 @@ def tile_acd_pa_t_kernel(tc, x, q_w, q_b, k_w, k_b, out_0, out_1, out_2):
                         gates(s - 1)
                         if s + 1 < B:
                             scalar_path(s + 1)
-                        if s + 3 < B:
-                            x_regroup(s + 3)
                 if s < B:
                     empty(s, idx)
                     fill_next()
             if s >= 2 and (s - 2) not in VECTOR_BATCHES:
-                product_rest(s - 2)
+                product(nc.vector, s - 2, GPSIMD_COLUMNS, N)
                 store_enhanced(s - 2)
             if s < B:
                 if s + 2 < B:

@@ -17,7 +17,7 @@ B, C, N, HEADS, HD = 16, 512, 256, 2, 512
 PACK = 4
 FLOPS = 2 * B * HEADS * 2 * N * C * HD + 2 * B * HEADS * N * N * HD
 VECTOR_BATCHES = (14, 15)
-GPSIMD_COLUMNS = 176
+GPSIMD_COLUMNS = 200
 SCALAR_MATRIX = 3
 
 
@@ -31,16 +31,15 @@ def tile_acd_pa_t_kernel(tc, x, q_w, q_b, k_w, k_b, out_0, out_1, out_2):
         ctx.enter_context(tc.manual_schedule())
 
         w_dram = (q_w[0], k_w[0], q_w[1], k_w[1])
-        w_raw = [const.tile([P, PACK, C], BF16, name="w_raw%d" % m) for m in range(4)]
+        w_raw = [[const.tile([P, 2, C], BF16, name="w_raw%d_%d" % (m, half)) for half in range(2)] for m in range(4)]
         x_raw = [const.tile([P, PACK, N], BF16, name="x_raw%d" % b) for b in range(B)]
         qb_bf = const.tile([P, HEADS, PACK], BF16, name="qb_bf")
         kb_bf = const.tile([P, HEADS, PACK], BF16, name="kb_bf")
 
         def load_w(m):
-            nc.sync.dma_start(
-                out=w_raw[m][:].rearrange("p t c -> p (t c)"),
-                in_=w_dram[m].rearrange("(p t) c -> p (t c)", t=PACK),
-            )
+            rows = w_dram[m].rearrange("(p t) c -> p t c", t=PACK)
+            for half in range(2):
+                nc.sync.dma_start(out=w_raw[m][half][:], in_=rows[:, 2 * half : 2 * half + 2, :])
 
         def load_x(b):
             nc.sync.dma_start(
@@ -51,11 +50,11 @@ def tile_acd_pa_t_kernel(tc, x, q_w, q_b, k_w, k_b, out_0, out_1, out_2):
         with nc.allow_non_contiguous_dma(reason="bias: four neighbouring values to a partition"):
             nc.scalar.dma_start(out=qb_bf[:], in_=q_b.rearrange("h (p t) -> p h t", t=PACK))
             nc.scalar.dma_start(out=kb_bf[:], in_=k_b.rearrange("h (p t) -> p h t", t=PACK))
-        load_w(0)
         load_x(0)
+        load_w(0)
         load_w(1)
-        load_x(1)
         load_w(2)
+        load_x(1)
         load_w(3)
         for b in range(2, B):
             load_x(b)
@@ -76,12 +75,12 @@ def tile_acd_pa_t_kernel(tc, x, q_w, q_b, k_w, k_b, out_0, out_1, out_2):
         w_grouped = {}
 
         def w_transpose(m):
-            words = w_raw[m][:].bitcast(F32)
             for half in range(2):
+                words = w_raw[m][half][:].bitcast(F32)
                 bank = psum.tile([P, 2, 2, P], F32, name="w_bank", tag=("sim" if m % 2 == 0 else "sq"), bufs=2)
                 for tt in range(2):
                     for u in range(2):
-                        nc.tensor.transpose(bank[:, tt, u, :], words[:, 2 * half + tt, u : C // 2 : 2], ident[:])
+                        nc.tensor.transpose(bank[:, tt, u, :], words[:, tt, u : C // 2 : 2], ident[:])
                 w_banks[(m, half)] = bank
 
         def w_empty(m, on_vector):
@@ -98,8 +97,6 @@ def tile_acd_pa_t_kernel(tc, x, q_w, q_b, k_w, k_b, out_0, out_1, out_2):
 
         def w_quantise(m):
             flat = w_grouped[m][:].rearrange("p t d j -> p (t d j)")
-            if m == 3:
-                nc.vector.tensor_scalar_mul(out=flat, in0=flat, scalar1=-1.0)
             nc.vector.quantize_mx(out=w_codes[m][:].bitcast(FP8X4), scales=w_scales[m][:], in_=flat)
 
         x_grouped = {}
@@ -187,7 +184,7 @@ def tile_acd_pa_t_kernel(tc, x, q_w, q_b, k_w, k_b, out_0, out_1, out_2):
                     in_=sq[t // 2][:, t % 2, :],
                     func=ACT.Identity,
                     bias=bias_f[:, m // 2, m % 2, t : t + 1],
-                    scale=1.0,
+                    scale=-1.0,
                 )
             nc.scalar.copy(
                 out=grouped_of(b)[:, m].rearrange("p (c i) t -> p c t i", i=4),
@@ -197,12 +194,13 @@ def tile_acd_pa_t_kernel(tc, x, q_w, q_b, k_w, k_b, out_0, out_1, out_2):
         def empty(b, i):
             m, nh = i // 2, i % 2
             grouped_of(b)
-            nc.vector.tensor_tensor(
-                out=qk_grouped[b][:, m, nh * P : (nh + 1) * P, :],
-                in0=banks[(b, i)][:].rearrange("p t c -> p c t"),
-                in1=bias_f[:, m // 2, m % 2, :].unsqueeze(1).to_broadcast([P, P, PACK]),
-                op=ALU.add,
-            )
+            sums = banks[(b, i)][:].rearrange("p t c -> p c t")
+            bias = bias_f[:, m // 2, m % 2, :].unsqueeze(1).to_broadcast([P, P, PACK])
+            dst = qk_grouped[b][:, m, nh * P : (nh + 1) * P, :]
+            if m == SCALAR_MATRIX:
+                nc.vector.tensor_tensor(out=dst, in0=bias, in1=sums, op=ALU.subtract)
+            else:
+                nc.vector.tensor_tensor(out=dst, in0=sums, in1=bias, op=ALU.add)
 
         def qk_quantise(b):
             qk_codes[b] = work.tile([P, 4 * N], U32, name="qk_codes", align_bytes=64)
@@ -275,28 +273,30 @@ def tile_acd_pa_t_kernel(tc, x, q_w, q_b, k_w, k_b, out_0, out_1, out_2):
                 in_=enhanced[b][:].rearrange("p h j n -> p h (j n)"),
             )
 
-        def product_vector(b):
+        def product_vector(b, pieces):
             enhanced_tile(b)
+            step = PACK // pieces
             for h in range(HEADS):
-                nc.vector.tensor_tensor(
-                    out=enhanced[b][:, h],
-                    in0=x_raw[b][:],
-                    in1=att[b][:, h, :].unsqueeze(1).to_broadcast([P, PACK, N]),
-                    op=ALU.mult,
-                )
-                nc.sync.dma_start(
-                    out=out_1[b, h * C : (h + 1) * C].rearrange("(p j) i w -> p (j i w)", j=PACK),
-                    in_=enhanced[b][:, h].rearrange("p j n -> p (j n)"),
-                )
+                for j0 in range(0, PACK, step):
+                    nc.vector.tensor_tensor(
+                        out=enhanced[b][:, h, j0 : j0 + step, :],
+                        in0=x_raw[b][:, j0 : j0 + step, :],
+                        in1=att[b][:, h, :].unsqueeze(1).to_broadcast([P, step, N]),
+                        op=ALU.mult,
+                    )
+                    nc.sync.dma_start(
+                        out=out_1[b, h * C : (h + 1) * C].rearrange("(p j) i w -> p j (i w)", j=PACK)[:, j0 : j0 + step, :],
+                        in_=enhanced[b][:, h, j0 : j0 + step, :],
+                    )
 
+        x_regroup(0)
+        x_quantise(0)
         w_transpose(0)
         w_empty(0, True)
-        x_regroup(0)
-        x_regroup(1)
         w_quantise(0)
-        x_quantise(0)
         w_transpose(1)
         w_empty(1, False)
+        x_regroup(1)
         fill_next()
         fill_next()
         w_transpose(2)
@@ -332,7 +332,7 @@ def tile_acd_pa_t_kernel(tc, x, q_w, q_b, k_w, k_b, out_0, out_1, out_2):
 
         for s in range(1, B + 2):
             if s >= 2 and (s - 2) in VECTOR_BATCHES:
-                product_vector(s - 2)
+                product_vector(s - 2, 1 if s - 2 < B - 1 else 2)
             if s >= 2 and (s - 2) not in VECTOR_BATCHES:
                 enhanced_tile(s - 2)
                 product(nc.gpsimd, s - 2, 0, GPSIMD_COLUMNS)

@@ -17,7 +17,7 @@ B, C, N, HEADS, HD = 16, 512, 256, 2, 512
 PACK = 4
 FLOPS = 2 * B * HEADS * 2 * N * C * HD + 2 * B * HEADS * N * N * HD
 VECTOR_BATCHES = (14, 15)
-GPSIMD_COLUMNS = 200
+GPSIMD_COLUMNS = 176
 SCALAR_MATRIX = 3
 
 
@@ -50,8 +50,8 @@ def tile_acd_pa_t_kernel(tc, x, q_w, q_b, k_w, k_b, out_0, out_1, out_2):
         with nc.allow_non_contiguous_dma(reason="bias: four neighbouring values to a partition"):
             nc.scalar.dma_start(out=qb_bf[:], in_=q_b.rearrange("h (p t) -> p h t", t=PACK))
             nc.scalar.dma_start(out=kb_bf[:], in_=k_b.rearrange("h (p t) -> p h t", t=PACK))
-        load_x(0)
         load_w(0)
+        load_x(0)
         load_w(1)
         load_w(2)
         load_x(1)
@@ -290,10 +290,10 @@ def tile_acd_pa_t_kernel(tc, x, q_w, q_b, k_w, k_b, out_0, out_1, out_2):
                     )
 
         x_regroup(0)
-        x_quantise(0)
         w_transpose(0)
         w_empty(0, True)
         w_quantise(0)
+        x_quantise(0)
         w_transpose(1)
         w_empty(1, False)
         x_regroup(1)
@@ -327,8 +327,8 @@ def tile_acd_pa_t_kernel(tc, x, q_w, q_b, k_w, k_b, out_0, out_1, out_2):
         for i in range(5, 8):
             empty(0, i)
             fill_next()
-        x_quantise(2)
         qk_quantise(0)
+        x_quantise(2)
 
         for s in range(1, B + 2):
             if s >= 2 and (s - 2) in VECTOR_BATCHES:
@@ -357,6 +357,6 @@ def tile_acd_pa_t_kernel(tc, x, q_w, q_b, k_w, k_b, out_0, out_1, out_2):
                 product(nc.vector, s - 2, GPSIMD_COLUMNS, N)
                 store_enhanced(s - 2)
             if s < B:
+                qk_quantise(s)
                 if s + 2 < B:
                     x_quantise(s + 2)
-                qk_quantise(s)

@@ -17,7 +17,8 @@ B, C, N, HEADS, HD = 16, 512, 256, 2, 512
 PACK = 4
 FLOPS = 2 * B * HEADS * 2 * N * C * HD + 2 * B * HEADS * N * N * HD
 VECTOR_BATCHES = (14, 15)
-GPSIMD_COLUMNS = 176
+GPSIMD_COLUMNS = 192
+VECTOR_COLUMNS = N - GPSIMD_COLUMNS
 SCALAR_MATRIX = 3
 
 
@@ -77,7 +78,7 @@ def tile_acd_pa_t_kernel(tc, x, q_w, q_b, k_w, k_b, out_0, out_1, out_2):
         def w_transpose(m):
             for half in range(2):
                 words = w_raw[m][half][:].bitcast(F32)
-                bank = psum.tile([P, 2, 2, P], F32, name="w_bank", tag=("sim" if m % 2 == 0 else "sq"), bufs=2)
+                bank = psum.tile([P, 2, 2, P], F32, name="w_bank", tag=("qk" if m == 1 else "out"), bufs=(4 if m == 1 else 3))
                 for tt in range(2):
                     for u in range(2):
                         nc.tensor.transpose(bank[:, tt, u, :], words[:, tt, u : C // 2 : 2], ident[:])
@@ -126,16 +127,18 @@ def tile_acd_pa_t_kernel(tc, x, q_w, q_b, k_w, k_b, out_0, out_1, out_2):
         qk_scales = {}
         sim_banks = {}
         dsum_sb = {}
-        dd_banks = {}
+        dd = psum.tile([P, 2, N], F32, name="dd", bufs=1)
         order = [(b, i) for b in range(B) for i in range(8 if b == 0 else 6)]
         state = {"next": 0}
         sim_sb = {}
         att = {}
+        att_psum = {}
+        planes = {}
         enhanced = {}
 
         def fill(b, i):
             m, nh = i // 2, i % 2
-            bank = psum.tile([P, PACK, P], F32, name="qk_bank", tag="qk", bufs=3)
+            bank = psum.tile([P, PACK, P], F32, name="qk_bank", tag="qk", bufs=4)
             banks[(b, i)] = bank
             cols = slice(nh * P, (nh + 1) * P)
             for t in range(PACK):
@@ -157,15 +160,15 @@ def tile_acd_pa_t_kernel(tc, x, q_w, q_b, k_w, k_b, out_0, out_1, out_2):
 
         def grouped_of(b):
             if b not in qk_grouped:
-                qk_grouped[b] = work.tile([P, 4, N, PACK], BF16, name="qk_grouped", tag="big%d" % (b % 3), bufs=1, align_bytes=64)
+                qk_grouped[b] = work.tile([P, 4, N, PACK], BF16, name="qk_grouped", tag="big%d" % (b % 4), bufs=1, align_bytes=64)
             return qk_grouped[b]
 
-        def scalar_path(b):
+        def scalar_planes(b):
             m = SCALAR_MATRIX
-            planes = work.tile([P, PACK, N], BF16, name="planes")
+            planes[b] = work.tile([P, PACK, N], BF16, name="planes")
             sq = []
             for th in range(2):
-                bank = psum.tile([P, 2, N], F32, name="sq_bank", tag="sq", bufs=2)
+                bank = psum.tile([P, 2, N], F32, name="sq_bank", tag="out", bufs=3)
                 sq.append(bank)
                 for tt in range(2):
                     t = 2 * th + tt
@@ -180,15 +183,17 @@ def tile_acd_pa_t_kernel(tc, x, q_w, q_b, k_w, k_b, out_0, out_1, out_2):
                     )
             for t in range(PACK):
                 nc.scalar.activation(
-                    out=planes[:, t, :],
+                    out=planes[b][:, t, :],
                     in_=sq[t // 2][:, t % 2, :],
                     func=ACT.Identity,
                     bias=bias_f[:, m // 2, m % 2, t : t + 1],
                     scale=-1.0,
                 )
+
+        def scalar_regroup(b):
             nc.scalar.copy(
-                out=grouped_of(b)[:, m].rearrange("p (c i) t -> p c t i", i=4),
-                in_=planes[:].rearrange("p t (c i) -> p c t i", i=4),
+                out=grouped_of(b)[:, SCALAR_MATRIX].rearrange("p (c i) t -> p c t i", i=4),
+                in_=planes[b][:].rearrange("p t (c i) -> p c t i", i=4),
             )
 
         def empty(b, i):
@@ -202,13 +207,15 @@ def tile_acd_pa_t_kernel(tc, x, q_w, q_b, k_w, k_b, out_0, out_1, out_2):
             else:
                 nc.vector.tensor_tensor(out=dst, in0=sums, in1=bias, op=ALU.add)
 
-        def qk_quantise(b):
-            qk_codes[b] = work.tile([P, 4 * N], U32, name="qk_codes", align_bytes=64)
-            qk_scales[b] = work.tile([P, 4 * N], U8, name="qk_scales", align_bytes=64)
+        def qk_quantise(b, h):
+            if h == 0:
+                qk_codes[b] = work.tile([P, 4 * N], U32, name="qk_codes", align_bytes=64)
+                qk_scales[b] = work.tile([P, 4 * N], U8, name="qk_scales", align_bytes=64)
+            cols = slice(2 * h * N, 2 * (h + 1) * N)
             nc.vector.quantize_mx(
-                out=qk_codes[b][:].bitcast(FP8X4),
-                scales=qk_scales[b][:],
-                in_=qk_grouped[b][:].rearrange("p m n j -> p (m n j)"),
+                out=qk_codes[b][:, cols].bitcast(FP8X4),
+                scales=qk_scales[b][:, cols],
+                in_=qk_grouped[b][:, 2 * h : 2 * h + 2].rearrange("p m n j -> p (m n j)"),
             )
 
         def sim_pass(b, h, qt, out, start, stop):
@@ -225,8 +232,6 @@ def tile_acd_pa_t_kernel(tc, x, q_w, q_b, k_w, k_b, out_0, out_1, out_2):
             )
 
         def stage2_sum(b):
-            dd = psum.tile([P, 2, N], F32, name="dd", tag="dd", bufs=1)
-            dd_banks[b] = dd
             for h in range(HEADS):
                 for qt in range(2):
                     sim_pass(b, h, qt, dd[:, 0, :], h == 0 and qt == 0, h == 1 and qt == 1)
@@ -234,7 +239,7 @@ def tile_acd_pa_t_kernel(tc, x, q_w, q_b, k_w, k_b, out_0, out_1, out_2):
             nc.scalar.copy(out=dsum_sb[b][:], in_=dd[:, 0, :])
 
         def stage2_sim(b, h):
-            bank = psum.tile([P, 2, N], F32, name="sim_bank", tag="sim", bufs=2)
+            bank = psum.tile([P, 2, N], F32, name="sim_bank", tag="out", bufs=3)
             for qt in range(2):
                 sim_pass(b, h, qt, bank[:, qt, :], True, True)
             if h == 0:
@@ -248,22 +253,35 @@ def tile_acd_pa_t_kernel(tc, x, q_w, q_b, k_w, k_b, out_0, out_1, out_2):
                     in_=sim_sb[b][:].rearrange("p h qt k -> p (h qt) k"),
                 )
 
-        def gates(b):
-            diff = dd_banks[b][:, 1, :]
-            nc.tensor.matmul(out=diff, lhsT=ones[:], rhs=dsum_sb[b][:], start=True, stop=True)
+        def column_sums(b):
+            nc.tensor.matmul(out=dd[:, 0, :], lhsT=ones[:], rhs=dsum_sb[b][:], start=True, stop=True)
+
+        def sigmoids(b):
+            diff = dd[:, 0, :]
             att[b] = work.tile([P, HEADS, N], F32, name="att", bufs=3)
             nc.scalar.activation(out=att[b][:, 0, :], in_=diff, func=ACT.Sigmoid, scale=inv_sqrt)
             nc.scalar.activation(out=att[b][:, 1, :], in_=diff, func=ACT.Sigmoid, scale=-inv_sqrt)
             nc.sync.dma_start(out=out_0[b : b + 1].rearrange("o h i j -> o h (i j)"), in_=att[b][0:1, :, :])
 
         def enhanced_tile(b):
-            enhanced[b] = work.tile([P, HEADS, PACK, N], F32, name="enhanced", tag="big%d" % ((b + 1) % 3), bufs=1, align_bytes=64)
+            enhanced[b] = work.tile([P, HEADS, PACK, N], F32, name="enhanced", tag="big%d" % ((b + 1) % 4), bufs=1, align_bytes=64)
 
-        def product(engine, b, lo, hi):
+        def att_to_psum(b):
+            spread = dd[:, 1, 0 : HEADS * VECTOR_COLUMNS].rearrange("p (h n) -> p h n", h=HEADS)
+            nc.tensor.matmul(
+                out=spread,
+                lhsT=ident[:, 0:1].to_broadcast([P, P]),
+                rhs=att[b][:, :, GPSIMD_COLUMNS:N],
+                start=True,
+                stop=True,
+            )
+            att_psum[b] = spread
+
+        def product(engine, b, lo, hi, gate):
             engine.tensor_tensor(
                 out=enhanced[b][:, :, :, lo:hi],
                 in0=x_raw[b][:, :, lo:hi].unsqueeze(1).to_broadcast([P, HEADS, PACK, hi - lo]),
-                in1=att[b][:, :, lo:hi].unsqueeze(2).to_broadcast([P, HEADS, PACK, hi - lo]),
+                in1=gate.unsqueeze(2).to_broadcast([P, HEADS, PACK, hi - lo]),
                 op=ALU.mult,
             )
 
@@ -322,41 +340,53 @@ def tile_acd_pa_t_kernel(tc, x, q_w, q_b, k_w, k_b, out_0, out_1, out_2):
         fill_next()
         empty(0, 4)
         fill_next()
-        scalar_path(1)
+        scalar_planes(1)
+        scalar_regroup(1)
         x_regroup(3)
         for i in range(5, 8):
             empty(0, i)
             fill_next()
-        qk_quantise(0)
+        fill_next()
+        qk_quantise(0, 0)
+        qk_quantise(0, 1)
         x_quantise(2)
 
         for s in range(1, B + 2):
-            if s >= 2 and (s - 2) in VECTOR_BATCHES:
+            shared = s >= 2 and (s - 2) not in VECTOR_BATCHES
+            if s >= 2 and not shared:
                 product_vector(s - 2, 1 if s - 2 < B - 1 else 2)
-            if s >= 2 and (s - 2) not in VECTOR_BATCHES:
+            if shared:
                 enhanced_tile(s - 2)
-                product(nc.gpsimd, s - 2, 0, GPSIMD_COLUMNS)
-            for idx in range(6):
-                if s <= B:
+                product(nc.gpsimd, s - 2, 0, GPSIMD_COLUMNS, att[s - 2][:, :, 0:GPSIMD_COLUMNS])
+            if s == B:
+                stage2_sim(s - 1, 0)
+                stage2_sum(s - 1)
+                column_sums(s - 1)
+                sigmoids(s - 1)
+                stage2_sim(s - 1, 1)
+            if s < B:
+                for idx in range(6):
                     if idx == 0:
                         stage2_sum(s - 1)
+                        stage2_sim(s - 1, 0)
                         if s + 3 < B:
                             x_regroup(s + 3)
-                    if idx == 1:
-                        stage2_sim(s - 1, 0)
                     if idx == 2:
+                        column_sums(s - 1)
+                        if shared:
+                            att_to_psum(s - 2)
+                        sigmoids(s - 1)
                         stage2_sim(s - 1, 1)
                     if idx == 3:
-                        gates(s - 1)
                         if s + 1 < B:
-                            scalar_path(s + 1)
-                if s < B:
+                            scalar_planes(s + 1)
+                            scalar_regroup(s + 1)
                     empty(s, idx)
                     fill_next()
-            if s >= 2 and (s - 2) not in VECTOR_BATCHES:
-                product(nc.vector, s - 2, GPSIMD_COLUMNS, N)
-                store_enhanced(s - 2)
-            if s < B:
-                qk_quantise(s)
+                qk_quantise(s, 0)
+                if shared:
+                    product(nc.vector, s - 2, GPSIMD_COLUMNS, N, att_psum[s - 2])
+                    store_enhanced(s - 2)
+                qk_quantise(s, 1)
                 if s + 2 < B:
                     x_quantise(s + 2)

@@ -16,10 +16,10 @@ P = 128
 B, C, N, HEADS, HD = 16, 512, 256, 2, 512
 PACK = 4
 FLOPS = 2 * B * HEADS * 2 * N * C * HD + 2 * B * HEADS * N * N * HD
-VECTOR_BATCHES = (14, 15)
+LAST_BATCHES = (14, 15)
 GPSIMD_COLUMNS = 192
 VECTOR_COLUMNS = N - GPSIMD_COLUMNS
-SCALAR_MATRIX = 3
+NEGATED = 3
 
 
 def tile_acd_pa_t_kernel(tc, x, q_w, q_b, k_w, k_b, out_0, out_1, out_2):
@@ -62,6 +62,8 @@ def tile_acd_pa_t_kernel(tc, x, q_w, q_b, k_w, k_b, out_0, out_1, out_2):
 
         ident = const.tile([P, P], F32, name="ident")
         make_identity(nc, ident[:])
+        ident_bf = const.tile([P, P], BF16, name="ident_bf")
+        make_identity(nc, ident_bf[:])
         ones = const.tile([P, P], F32, name="ones")
         nc.vector.memset(ones[:], 1.0)
         warm_in = const.tile([P, 1], F32, name="warm_in")
@@ -75,26 +77,23 @@ def tile_acd_pa_t_kernel(tc, x, q_w, q_b, k_w, k_b, out_0, out_1, out_2):
         w_banks = {}
         w_grouped = {}
 
-        def w_transpose(m):
-            for half in range(2):
-                words = w_raw[m][half][:].bitcast(F32)
-                bank = psum.tile([P, 2, 2, P], F32, name="w_bank", tag=("qk" if m == 1 else "out"), bufs=(4 if m == 1 else 3))
-                for tt in range(2):
-                    for u in range(2):
-                        nc.tensor.transpose(bank[:, tt, u, :], words[:, tt, u : C // 2 : 2], ident[:])
-                w_banks[(m, half)] = bank
+        def w_transpose(m, half):
+            words = w_raw[m][half][:].bitcast(F32)
+            bank = psum.tile([P, 2, 2, P], F32, name="w_bank", tag=("qk" if m % 2 == 1 else "out"), bufs=(4 if m % 2 == 1 else 2))
+            for tt in range(2):
+                for u in range(2):
+                    nc.tensor.transpose(bank[:, tt, u, :], words[:, tt, u : C // 2 : 2], ident[:])
+            w_banks[(m, half)] = bank
 
-        def w_empty(m, on_vector):
-            grouped = work.tile([P, PACK, P, PACK], BF16, name="w_grouped", align_bytes=64)
-            w_grouped[m] = grouped
-            grouped_words = grouped[:].bitcast(F32)
-            for half in range(2):
-                dst = grouped_words[:, 2 * half : 2 * half + 2, :, :]
-                src = w_banks[(m, half)][:].rearrange("p t u d -> p t d u")
-                if on_vector:
-                    nc.vector.tensor_copy(out=dst, in_=src)
-                else:
-                    nc.scalar.copy(out=dst, in_=src)
+        def w_empty(m, half, on_vector):
+            if half == 0:
+                w_grouped[m] = work.tile([P, PACK, P, PACK], BF16, name="w_grouped", bufs=4, align_bytes=64)
+            dst = w_grouped[m][:].bitcast(F32)[:, 2 * half : 2 * half + 2, :, :]
+            src = w_banks[(m, half)][:].rearrange("p t u d -> p t d u")
+            if on_vector:
+                nc.vector.tensor_copy(out=dst, in_=src)
+            else:
+                nc.scalar.copy(out=dst, in_=src)
 
         def w_quantise(m):
             flat = w_grouped[m][:].rearrange("p t d j -> p (t d j)")
@@ -105,10 +104,9 @@ def tile_acd_pa_t_kernel(tc, x, q_w, q_b, k_w, k_b, out_0, out_1, out_2):
         x_scales = {}
 
         def x_regroup(b):
-            grouped = work.tile([P, N, PACK], BF16, name="x_grouped", bufs=3, align_bytes=64)
-            x_grouped[b] = grouped
+            x_grouped[b] = work.tile([P, N, PACK], BF16, name="x_grouped", bufs=3, align_bytes=64)
             nc.scalar.copy(
-                out=grouped[:].rearrange("p (c i) t -> p c t i", i=4),
+                out=x_grouped[b][:].rearrange("p (c i) t -> p c t i", i=4),
                 in_=x_raw[b][:].rearrange("p t (c i) -> p c t i", i=4),
             )
 
@@ -127,13 +125,17 @@ def tile_acd_pa_t_kernel(tc, x, q_w, q_b, k_w, k_b, out_0, out_1, out_2):
         qk_scales = {}
         sim_banks = {}
         dsum_sb = {}
-        dd = psum.tile([P, 2, N], F32, name="dd", bufs=1)
+        dd_bank = psum.tile([P, 2 * N], F32, name="dd_bank", bufs=1)
+        dd = dd_bank[:, 0:N]
+        x_bank = psum.tile([P, 2 * N], F32, name="x_bank", bufs=1)
+        x_psum = x_bank[:, 0 : PACK * VECTOR_COLUMNS].rearrange("p (j n) -> p j n", j=PACK)
         order = [(b, i) for b in range(B) for i in range(8 if b == 0 else 6)]
         state = {"next": 0}
         sim_sb = {}
         att = {}
-        att_psum = {}
         planes = {}
+        x_full = {}
+        sq_banks = {}
         enhanced = {}
 
         def fill(b, i):
@@ -163,37 +165,38 @@ def tile_acd_pa_t_kernel(tc, x, q_w, q_b, k_w, k_b, out_0, out_1, out_2):
                 qk_grouped[b] = work.tile([P, 4, N, PACK], BF16, name="qk_grouped", tag="big%d" % (b % 4), bufs=1, align_bytes=64)
             return qk_grouped[b]
 
-        def scalar_planes(b):
-            m = SCALAR_MATRIX
-            planes[b] = work.tile([P, PACK, N], BF16, name="planes")
-            sq = []
-            for th in range(2):
-                bank = psum.tile([P, 2, N], F32, name="sq_bank", tag="out", bufs=3)
-                sq.append(bank)
-                for tt in range(2):
-                    t = 2 * th + tt
-                    nc.tensor.matmul_mx(
-                        out=bank[:, tt, :],
-                        lhsT=w_codes[m][:, t * P : (t + 1) * P].bitcast(FP8X4),
-                        lhsT_scale=w_scales[m][:, t * P : (t + 1) * P],
-                        rhs=x_codes[b][:].bitcast(FP8X4),
-                        rhs_scale=x_scales[b][:],
-                        start=True,
-                        stop=True,
-                    )
-            for t in range(PACK):
-                nc.scalar.activation(
-                    out=planes[b][:, t, :],
-                    in_=sq[t // 2][:, t % 2, :],
-                    func=ACT.Identity,
-                    bias=bias_f[:, m // 2, m % 2, t : t + 1],
-                    scale=-1.0,
+        def scalar_pass(b, m, th):
+            bank = psum.tile([P, 2, N], F32, name="sq_bank", tag="out", bufs=2)
+            sq_banks[(b, m, th)] = bank
+            for tt in range(2):
+                t = 2 * th + tt
+                nc.tensor.matmul_mx(
+                    out=bank[:, tt, :],
+                    lhsT=w_codes[m][:, t * P : (t + 1) * P].bitcast(FP8X4),
+                    lhsT_scale=w_scales[m][:, t * P : (t + 1) * P],
+                    rhs=x_codes[b][:].bitcast(FP8X4),
+                    rhs_scale=x_scales[b][:],
+                    start=True,
+                    stop=True,
                 )
 
-        def scalar_regroup(b):
+        def scalar_planes(b, m, th):
+            if th == 0:
+                planes[(b, m)] = work.tile([P, PACK, N], BF16, name="planes", bufs=3)
+            for tt in range(2):
+                t = 2 * th + tt
+                nc.scalar.activation(
+                    out=planes[(b, m)][:, t, :],
+                    in_=sq_banks[(b, m, th)][:, tt, :],
+                    func=ACT.Identity,
+                    bias=bias_f[:, m // 2, m % 2, t : t + 1],
+                    scale=-1.0 if m == NEGATED else 1.0,
+                )
+
+        def scalar_regroup(b, m):
             nc.scalar.copy(
-                out=grouped_of(b)[:, SCALAR_MATRIX].rearrange("p (c i) t -> p c t i", i=4),
-                in_=planes[b][:].rearrange("p t (c i) -> p c t i", i=4),
+                out=grouped_of(b)[:, m].rearrange("p (c i) t -> p c t i", i=4),
+                in_=planes[(b, m)][:].rearrange("p t (c i) -> p c t i", i=4),
             )
 
         def empty(b, i):
@@ -202,7 +205,7 @@ def tile_acd_pa_t_kernel(tc, x, q_w, q_b, k_w, k_b, out_0, out_1, out_2):
             sums = banks[(b, i)][:].rearrange("p t c -> p c t")
             bias = bias_f[:, m // 2, m % 2, :].unsqueeze(1).to_broadcast([P, P, PACK])
             dst = qk_grouped[b][:, m, nh * P : (nh + 1) * P, :]
-            if m == SCALAR_MATRIX:
+            if m == NEGATED:
                 nc.vector.tensor_tensor(out=dst, in0=bias, in1=sums, op=ALU.subtract)
             else:
                 nc.vector.tensor_tensor(out=dst, in0=sums, in1=bias, op=ALU.add)
@@ -231,17 +234,22 @@ def tile_acd_pa_t_kernel(tc, x, q_w, q_b, k_w, k_b, out_0, out_1, out_2):
                 stop=stop,
             )
 
-        def stage2_sum(b):
+        def sum_passes(b):
             for h in range(HEADS):
                 for qt in range(2):
-                    sim_pass(b, h, qt, dd[:, 0, :], h == 0 and qt == 0, h == 1 and qt == 1)
-            dsum_sb[b] = work.tile([P, N], F32, name="dsum_sb")
-            nc.scalar.copy(out=dsum_sb[b][:], in_=dd[:, 0, :])
+                    sim_pass(b, h, qt, dd, h == 0 and qt == 0, h == 1 and qt == 1)
 
-        def stage2_sim(b, h):
-            bank = psum.tile([P, 2, N], F32, name="sim_bank", tag="out", bufs=3)
+        def sum_empty(b):
+            dsum_sb[b] = work.tile([P, N], F32, name="dsum_sb")
+            nc.scalar.copy(out=dsum_sb[b][:], in_=dd)
+
+        def sim_passes(b, h):
+            sim_banks[(b, h)] = psum.tile([P, 2, N], F32, name="sim_bank", tag="out", bufs=2)
             for qt in range(2):
-                sim_pass(b, h, qt, bank[:, qt, :], True, True)
+                sim_pass(b, h, qt, sim_banks[(b, h)][:, qt, :], True, True)
+
+        def sim_empty(b, h):
+            bank = sim_banks[(b, h)]
             if h == 0:
                 sim_sb[b] = work.tile([P, HEADS, 2, N], F32, name="sim_sb", bufs=3)
             nc.scalar.activation(
@@ -254,139 +262,187 @@ def tile_acd_pa_t_kernel(tc, x, q_w, q_b, k_w, k_b, out_0, out_1, out_2):
                 )
 
         def column_sums(b):
-            nc.tensor.matmul(out=dd[:, 0, :], lhsT=ones[:], rhs=dsum_sb[b][:], start=True, stop=True)
+            nc.tensor.matmul(out=dd, lhsT=ones[:], rhs=dsum_sb[b][:], start=True, stop=True)
 
         def sigmoids(b):
-            diff = dd[:, 0, :]
+            diff = dd
             att[b] = work.tile([P, HEADS, N], F32, name="att", bufs=3)
             nc.scalar.activation(out=att[b][:, 0, :], in_=diff, func=ACT.Sigmoid, scale=inv_sqrt)
             nc.scalar.activation(out=att[b][:, 1, :], in_=diff, func=ACT.Sigmoid, scale=-inv_sqrt)
+
+        def store_att(b):
             nc.sync.dma_start(out=out_0[b : b + 1].rearrange("o h i j -> o h (i j)"), in_=att[b][0:1, :, :])
 
         def enhanced_tile(b):
             enhanced[b] = work.tile([P, HEADS, PACK, N], F32, name="enhanced", tag="big%d" % ((b + 1) % 4), bufs=1, align_bytes=64)
 
-        def att_to_psum(b):
-            spread = dd[:, 1, 0 : HEADS * VECTOR_COLUMNS].rearrange("p (h n) -> p h n", h=HEADS)
+        def x_share(b):
             nc.tensor.matmul(
-                out=spread,
-                lhsT=ident[:, 0:1].to_broadcast([P, P]),
-                rhs=att[b][:, :, GPSIMD_COLUMNS:N],
+                out=x_psum,
+                lhsT=ident_bf[:],
+                rhs=x_raw[b][:, :, GPSIMD_COLUMNS:N],
                 start=True,
                 stop=True,
             )
-            att_psum[b] = spread
 
-        def product(engine, b, lo, hi, gate):
+        def product(engine, b, lo, hi, values, heads):
             engine.tensor_tensor(
-                out=enhanced[b][:, :, :, lo:hi],
-                in0=x_raw[b][:, :, lo:hi].unsqueeze(1).to_broadcast([P, HEADS, PACK, hi - lo]),
-                in1=gate.unsqueeze(2).to_broadcast([P, HEADS, PACK, hi - lo]),
+                out=enhanced[b][:, heads, :, lo:hi],
+                in0=values.unsqueeze(1).to_broadcast([P, heads.stop - heads.start, PACK, hi - lo]),
+                in1=att[b][:, heads, lo:hi].unsqueeze(2).to_broadcast([P, heads.stop - heads.start, PACK, hi - lo]),
                 op=ALU.mult,
             )
 
-        def store_enhanced(b):
+        def product_gpsimd(b, heads):
+            product(nc.gpsimd, b, 0, GPSIMD_COLUMNS, x_raw[b][:, :, 0:GPSIMD_COLUMNS], heads)
+
+        def product_shared(b):
+            product(nc.vector, b, GPSIMD_COLUMNS, N, x_psum, slice(0, HEADS))
+
+        def store_enhanced(b, heads):
             nc.sync.dma_start(
-                out=out_1[b].rearrange("(h p j) i w -> p h (j i w)", h=HEADS, j=PACK),
-                in_=enhanced[b][:].rearrange("p h j n -> p h (j n)"),
+                out=out_1[b].rearrange("(h p j) i w -> p h (j i w)", h=HEADS, j=PACK)[:, heads, :],
+                in_=enhanced[b][:, heads].rearrange("p h j n -> p h (j n)"),
             )
 
-        def product_vector(b, pieces):
+        def x_to_psum(b):
+            x_full[b] = psum.tile([P, PACK, N], BF16, name="x_full", tag="qk", bufs=4)
+            for j0 in (0, 2):
+                nc.tensor.matmul(
+                    out=x_full[b][:, j0 : j0 + 2, :], lhsT=ident_bf[:], rhs=x_raw[b][:, j0 : j0 + 2, :], start=True, stop=True
+                )
+
+        def last_products(b):
             enhanced_tile(b)
-            step = PACK // pieces
-            for h in range(HEADS):
-                for j0 in range(0, PACK, step):
-                    nc.vector.tensor_tensor(
-                        out=enhanced[b][:, h, j0 : j0 + step, :],
-                        in0=x_raw[b][:, j0 : j0 + step, :],
-                        in1=att[b][:, h, :].unsqueeze(1).to_broadcast([P, step, N]),
-                        op=ALU.mult,
-                    )
-                    nc.sync.dma_start(
-                        out=out_1[b, h * C : (h + 1) * C].rearrange("(p j) i w -> p j (i w)", j=PACK)[:, j0 : j0 + step, :],
-                        in_=enhanced[b][:, h, j0 : j0 + step, :],
-                    )
+            for engine, values, h, j0 in (
+                (nc.gpsimd, x_raw[b], 1, 2),
+                (nc.vector, x_full[b], 0, 0),
+                (nc.vector, x_full[b], 0, 2),
+                (nc.vector, x_full[b], 1, 0),
+            ):
+                engine.tensor_tensor(
+                    out=enhanced[b][:, h, j0 : j0 + 2, :],
+                    in0=values[:, j0 : j0 + 2, :],
+                    in1=att[b][:, h, :].unsqueeze(1).to_broadcast([P, 2, N]),
+                    op=ALU.mult,
+                )
+            for h, j0 in ((0, 0), (0, 2), (1, 2), (1, 0)):
+                nc.sync.dma_start(
+                    out=out_1[b, h * C : (h + 1) * C].rearrange("(p j) i w -> p j (i w)", j=PACK)[:, j0 : j0 + 2, :],
+                    in_=enhanced[b][:, h, j0 : j0 + 2, :],
+                )
 
         x_regroup(0)
-        w_transpose(0)
-        w_empty(0, True)
+        w_transpose(0, 0)
+        w_transpose(0, 1)
+        w_empty(0, 0, True)
+        w_empty(0, 1, True)
         w_quantise(0)
         x_quantise(0)
-        w_transpose(1)
-        w_empty(1, False)
-        x_regroup(1)
+        w_transpose(1, 0)
+        w_transpose(1, 1)
+        w_empty(1, 0, False)
+        w_empty(1, 1, False)
+        w_transpose(2, 0)
         fill_next()
         fill_next()
-        w_transpose(2)
-        w_empty(2, False)
+        w_transpose(2, 1)
+        w_empty(2, 0, False)
+        w_empty(2, 1, False)
         nc.vector.tensor_copy(out=bias_f[:, :, 0, :], in_=qb_bf[:])
         nc.vector.tensor_copy(out=bias_f[:, 0, 1, :], in_=kb_bf[:, 0, :])
         nc.vector.tensor_scalar_mul(out=bias_f[:, 1, 1, :], in0=kb_bf[:, 1, :], scalar1=-1.0)
         empty(0, 0)
         w_quantise(1)
-        fill_next()
-        fill_next()
-        w_transpose(3)
-        w_empty(3, False)
-        x_regroup(2)
+        x_regroup(1)
+        w_transpose(3, 0)
+        w_transpose(3, 1)
+        w_empty(3, 0, False)
+        w_empty(3, 1, False)
         empty(0, 1)
-        x_quantise(1)
-        empty(0, 2)
+        fill_next()
+        fill_next()
         w_quantise(2)
         fill_next()
+        empty(0, 2)
+        x_quantise(1)
         fill_next()
         empty(0, 3)
         w_quantise(3)
-        fill_next()
+        x_regroup(2)
         empty(0, 4)
         fill_next()
-        scalar_planes(1)
-        scalar_regroup(1)
+        fill_next()
+        scalar_pass(1, 3, 0)
+        scalar_pass(1, 3, 1)
+        scalar_planes(1, 3, 0)
+        scalar_planes(1, 3, 1)
         x_regroup(3)
-        for i in range(5, 8):
-            empty(0, i)
-            fill_next()
+        empty(0, 5)
+        fill_next()
         fill_next()
         qk_quantise(0, 0)
+        empty(0, 6)
+        fill_next()
+        empty(0, 7)
+        fill_next()
         qk_quantise(0, 1)
         x_quantise(2)
 
         for s in range(1, B + 2):
-            shared = s >= 2 and (s - 2) not in VECTOR_BATCHES
-            if s >= 2 and not shared:
-                product_vector(s - 2, 1 if s - 2 < B - 1 else 2)
-            if shared:
+            if 2 <= s < B:
+                head_runs = [slice(0, HEADS)] if s < B - 1 else [slice(h, h + 1) for h in range(HEADS)]
                 enhanced_tile(s - 2)
-                product(nc.gpsimd, s - 2, 0, GPSIMD_COLUMNS, att[s - 2][:, :, 0:GPSIMD_COLUMNS])
+                for heads in head_runs:
+                    product_gpsimd(s - 2, heads)
+            if s >= B:
+                last_products(s - 2)
             if s == B:
-                stage2_sim(s - 1, 0)
-                stage2_sum(s - 1)
+                sim_passes(s - 1, 0)
+                sim_empty(s - 1, 0)
+                sum_passes(s - 1)
+                sum_empty(s - 1)
+                sim_passes(s - 1, 1)
+                sim_empty(s - 1, 1)
+                x_to_psum(s - 1)
                 column_sums(s - 1)
                 sigmoids(s - 1)
-                stage2_sim(s - 1, 1)
+                store_att(s - 1)
             if s < B:
                 for idx in range(6):
                     if idx == 0:
-                        stage2_sum(s - 1)
-                        stage2_sim(s - 1, 0)
+                        sim_passes(s - 1, 0)
+                        sim_empty(s - 1, 0)
+                        sim_passes(s - 1, 1)
+                        sim_empty(s - 1, 1)
+                        if s >= 2:
+                            x_share(s - 2)
+                        sum_passes(s - 1)
+                        sum_empty(s - 1)
+                        if s + 1 < B:
+                            scalar_pass(s + 1, 3, 0)
+                            scalar_planes(s + 1, 3, 0)
+                    if idx == 1:
+                        if s + 1 < B:
+                            scalar_pass(s + 1, 3, 1)
+                            scalar_planes(s + 1, 3, 1)
+                        scalar_regroup(s, 3)
+                    if idx == 2:
+                        if s >= 2:
+                            product_shared(s - 2)
+                        column_sums(s - 1)
+                        sigmoids(s - 1)
                         if s + 3 < B:
                             x_regroup(s + 3)
-                    if idx == 2:
-                        column_sums(s - 1)
-                        if shared:
-                            att_to_psum(s - 2)
-                        sigmoids(s - 1)
-                        stage2_sim(s - 1, 1)
-                    if idx == 3:
-                        if s + 1 < B:
-                            scalar_planes(s + 1)
-                            scalar_regroup(s + 1)
                     empty(s, idx)
                     fill_next()
+                if s >= 2:
+                    for heads in head_runs:
+                        store_enhanced(s - 2, heads)
+                store_att(s - 1)
                 qk_quantise(s, 0)
-                if shared:
-                    product(nc.vector, s - 2, GPSIMD_COLUMNS, N, att_psum[s - 2])
-                    store_enhanced(s - 2)
                 qk_quantise(s, 1)
                 if s + 2 < B:
                     x_quantise(s + 2)
+                if s == B - 1:
+                    x_to_psum(s - 1)

@@ -17,7 +17,7 @@ B, C, N, HEADS, HD = 16, 512, 256, 2, 512
 PACK = 4
 FLOPS = 2 * B * HEADS * 2 * N * C * HD + 2 * B * HEADS * N * N * HD
 LAST_BATCHES = (14, 15)
-GPSIMD_COLUMNS = 192
+GPSIMD_COLUMNS = 200
 VECTOR_COLUMNS = N - GPSIMD_COLUMNS
 NEGATED = 3
 
@@ -210,15 +210,15 @@ def tile_acd_pa_t_kernel(tc, x, q_w, q_b, k_w, k_b, out_0, out_1, out_2):
             else:
                 nc.vector.tensor_tensor(out=dst, in0=sums, in1=bias, op=ALU.add)
 
-        def qk_quantise(b, h):
-            if h == 0:
+        def qk_quantise(b, first, last):
+            if b not in qk_codes:
                 qk_codes[b] = work.tile([P, 4 * N], U32, name="qk_codes", align_bytes=64)
                 qk_scales[b] = work.tile([P, 4 * N], U8, name="qk_scales", align_bytes=64)
-            cols = slice(2 * h * N, 2 * (h + 1) * N)
+            cols = slice(first * N, (last + 1) * N)
             nc.vector.quantize_mx(
                 out=qk_codes[b][:, cols].bitcast(FP8X4),
                 scales=qk_scales[b][:, cols],
-                in_=qk_grouped[b][:, 2 * h : 2 * h + 2].rearrange("p m n j -> p (m n j)"),
+                in_=qk_grouped[b][:, first : last + 1].rearrange("p m n j -> p (m n j)"),
             )
 
         def sim_pass(b, h, qt, out, start, stop):
@@ -234,10 +234,9 @@ def tile_acd_pa_t_kernel(tc, x, q_w, q_b, k_w, k_b, out_0, out_1, out_2):
                 stop=stop,
             )
 
-        def sum_passes(b):
-            for h in range(HEADS):
-                for qt in range(2):
-                    sim_pass(b, h, qt, dd, h == 0 and qt == 0, h == 1 and qt == 1)
+        def sum_passes(b, h):
+            for qt in range(2):
+                sim_pass(b, h, qt, dd, h == 0 and qt == 0, h == 1 and qt == 1)
 
         def sum_empty(b):
             dsum_sb[b] = work.tile([P, N], F32, name="dsum_sb")
@@ -337,6 +336,9 @@ def tile_acd_pa_t_kernel(tc, x, q_w, q_b, k_w, k_b, out_0, out_1, out_2):
         w_transpose(0, 1)
         w_empty(0, 0, True)
         w_empty(0, 1, True)
+        nc.vector.tensor_copy(out=bias_f[:, :, 0, :], in_=qb_bf[:])
+        nc.vector.tensor_copy(out=bias_f[:, 0, 1, :], in_=kb_bf[:, 0, :])
+        nc.vector.tensor_scalar_mul(out=bias_f[:, 1, 1, :], in0=kb_bf[:, 1, :], scalar1=-1.0)
         w_quantise(0)
         x_quantise(0)
         w_transpose(1, 0)
@@ -349,26 +351,23 @@ def tile_acd_pa_t_kernel(tc, x, q_w, q_b, k_w, k_b, out_0, out_1, out_2):
         w_transpose(2, 1)
         w_empty(2, 0, False)
         w_empty(2, 1, False)
-        nc.vector.tensor_copy(out=bias_f[:, :, 0, :], in_=qb_bf[:])
-        nc.vector.tensor_copy(out=bias_f[:, 0, 1, :], in_=kb_bf[:, 0, :])
-        nc.vector.tensor_scalar_mul(out=bias_f[:, 1, 1, :], in0=kb_bf[:, 1, :], scalar1=-1.0)
         empty(0, 0)
         w_quantise(1)
-        x_regroup(1)
         w_transpose(3, 0)
         w_transpose(3, 1)
         w_empty(3, 0, False)
         w_empty(3, 1, False)
+        x_regroup(1)
         empty(0, 1)
         fill_next()
         fill_next()
         w_quantise(2)
         fill_next()
         empty(0, 2)
-        x_quantise(1)
+        w_quantise(3)
         fill_next()
         empty(0, 3)
-        w_quantise(3)
+        x_quantise(1)
         x_regroup(2)
         empty(0, 4)
         fill_next()
@@ -381,12 +380,12 @@ def tile_acd_pa_t_kernel(tc, x, q_w, q_b, k_w, k_b, out_0, out_1, out_2):
         empty(0, 5)
         fill_next()
         fill_next()
-        qk_quantise(0, 0)
         empty(0, 6)
         fill_next()
         empty(0, 7)
         fill_next()
-        qk_quantise(0, 1)
+        qk_quantise(0, 0, 1)
+        qk_quantise(0, 2, 3)
         x_quantise(2)
 
         for s in range(1, B + 2):
@@ -399,8 +398,9 @@ def tile_acd_pa_t_kernel(tc, x, q_w, q_b, k_w, k_b, out_0, out_1, out_2):
                 last_products(s - 2)
             if s == B:
                 sim_passes(s - 1, 0)
+                sum_passes(s - 1, 0)
                 sim_empty(s - 1, 0)
-                sum_passes(s - 1)
+                sum_passes(s - 1, 1)
                 sum_empty(s - 1)
                 sim_passes(s - 1, 1)
                 sim_empty(s - 1, 1)
@@ -411,13 +411,16 @@ def tile_acd_pa_t_kernel(tc, x, q_w, q_b, k_w, k_b, out_0, out_1, out_2):
             if s < B:
                 for idx in range(6):
                     if idx == 0:
+                        if s == B - 1:
+                            scalar_regroup(s, 3)
                         sim_passes(s - 1, 0)
                         sim_empty(s - 1, 0)
                         sim_passes(s - 1, 1)
                         sim_empty(s - 1, 1)
                         if s >= 2:
                             x_share(s - 2)
-                        sum_passes(s - 1)
+                        sum_passes(s - 1, 0)
+                        sum_passes(s - 1, 1)
                         sum_empty(s - 1)
                         if s + 1 < B:
                             scalar_pass(s + 1, 3, 0)
@@ -426,7 +429,7 @@ def tile_acd_pa_t_kernel(tc, x, q_w, q_b, k_w, k_b, out_0, out_1, out_2):
                         if s + 1 < B:
                             scalar_pass(s + 1, 3, 1)
                             scalar_planes(s + 1, 3, 1)
-                        scalar_regroup(s, 3)
+                            scalar_regroup(s, 3)
                     if idx == 2:
                         if s >= 2:
                             product_shared(s - 2)
@@ -440,9 +443,12 @@ def tile_acd_pa_t_kernel(tc, x, q_w, q_b, k_w, k_b, out_0, out_1, out_2):
                     for heads in head_runs:
                         store_enhanced(s - 2, heads)
                 store_att(s - 1)
-                qk_quantise(s, 0)
-                qk_quantise(s, 1)
+                qk_quantise(s, 0, 1)
+                if s < B - 1:
+                    qk_quantise(s, 2, 3)
+                else:
+                    qk_quantise(s, 3, 3)
+                    qk_quantise(s, 2, 2)
+                    x_to_psum(s - 1)
                 if s + 2 < B:
                     x_quantise(s + 2)
-                if s == B - 1:
-                    x_to_psum(s - 1)

@@ -60,6 +60,8 @@ def tile_acd_pa_t_kernel(tc, x, q_w, q_b, k_w, k_b, out_0, out_1, out_2):
         for b in range(2, B):
             load_x(b)
 
+        warm_operand = const.tile([P, 2 * N], BF16, name="warm_operand")
+        nc.vector.memset(warm_operand[:], 0.0)
         ident = const.tile([P, P], F32, name="ident")
         make_identity(nc, ident[:])
         ident_bf = const.tile([P, P], BF16, name="ident_bf")
@@ -98,6 +100,11 @@ def tile_acd_pa_t_kernel(tc, x, q_w, q_b, k_w, k_b, out_0, out_1, out_2):
         def w_quantise(m):
             flat = w_grouped[m][:].rearrange("p t d j -> p (t d j)")
             nc.vector.quantize_mx(out=w_codes[m][:].bitcast(FP8X4), scales=w_scales[m][:], in_=flat)
+
+        def warm_tensor(passes):
+            bank = psum.tile([P, 2 * N], F32, name="warm_bank", tag="qk", bufs=4)
+            for k in range(passes):
+                nc.tensor.matmul(out=bank[:], lhsT=warm_operand[:, 0:P], rhs=warm_operand[:], start=True, stop=True)
 
         x_grouped = {}
         x_codes = {}
@@ -332,8 +339,10 @@ def tile_acd_pa_t_kernel(tc, x, q_w, q_b, k_w, k_b, out_0, out_1, out_2):
                 )
 
         x_regroup(0)
+        warm_tensor(7)
         w_transpose(0, 0)
         w_transpose(0, 1)
+        warm_tensor(2)
         w_empty(0, 0, True)
         w_empty(0, 1, True)
         nc.vector.tensor_copy(out=bias_f[:, :, 0, :], in_=qb_bf[:])

@@ -48,12 +48,12 @@ def tile_acd_pa_t_kernel(tc, x, q_w, q_b, k_w, k_b, out_0, out_1, out_2):
                 in_=x[b].rearrange("(p j) h w -> p (j h w)", j=PACK),
             )
 
-        with nc.allow_non_contiguous_dma(reason="bias: four neighbouring values to a partition"):
-            nc.scalar.dma_start(out=qb_bf[:], in_=q_b.rearrange("h (p t) -> p h t", t=PACK))
-            nc.scalar.dma_start(out=kb_bf[:], in_=k_b.rearrange("h (p t) -> p h t", t=PACK))
         load_w(0)
         load_x(0)
         load_w(1)
+        with nc.allow_non_contiguous_dma(reason="bias: four neighbouring values to a partition"):
+            nc.sync.dma_start(out=qb_bf[:], in_=q_b.rearrange("h (p t) -> p h t", t=PACK))
+            nc.sync.dma_start(out=kb_bf[:], in_=k_b.rearrange("h (p t) -> p h t", t=PACK))
         load_w(2)
         load_x(1)
         load_w(3)
@@ -97,9 +97,13 @@ def tile_acd_pa_t_kernel(tc, x, q_w, q_b, k_w, k_b, out_0, out_1, out_2):
             else:
                 nc.scalar.copy(out=dst, in_=src)
 
-        def w_quantise(m):
-            flat = w_grouped[m][:].rearrange("p t d j -> p (t d j)")
-            nc.vector.quantize_mx(out=w_codes[m][:].bitcast(FP8X4), scales=w_scales[m][:], in_=flat)
+        def w_quantise(m, half):
+            cols = slice(half * 2 * P, (half + 1) * 2 * P)
+            nc.vector.quantize_mx(
+                out=w_codes[m][:, cols].bitcast(FP8X4),
+                scales=w_scales[m][:, cols],
+                in_=w_grouped[m][:, 2 * half : 2 * half + 2].rearrange("p t d j -> p (t d j)"),
+            )
 
         def warm_tensor(passes):
             bank = psum.tile([P, 2 * N], F32, name="warm_bank", tag="qk", bufs=4)
@@ -339,17 +343,18 @@ def tile_acd_pa_t_kernel(tc, x, q_w, q_b, k_w, k_b, out_0, out_1, out_2):
                 )
 
         x_regroup(0)
-        warm_tensor(7)
+        warm_tensor(3)
         w_transpose(0, 0)
         w_transpose(0, 1)
         warm_tensor(2)
         w_empty(0, 0, True)
         w_empty(0, 1, True)
+        w_quantise(0, 0)
+        w_quantise(0, 1)
+        x_quantise(0)
         nc.vector.tensor_copy(out=bias_f[:, :, 0, :], in_=qb_bf[:])
         nc.vector.tensor_copy(out=bias_f[:, 0, 1, :], in_=kb_bf[:, 0, :])
         nc.vector.tensor_scalar_mul(out=bias_f[:, 1, 1, :], in0=kb_bf[:, 1, :], scalar1=-1.0)
-        w_quantise(0)
-        x_quantise(0)
         w_transpose(1, 0)
         w_transpose(1, 1)
         w_empty(1, 0, False)
@@ -361,7 +366,8 @@ def tile_acd_pa_t_kernel(tc, x, q_w, q_b, k_w, k_b, out_0, out_1, out_2):
         w_empty(2, 0, False)
         w_empty(2, 1, False)
         empty(0, 0)
-        w_quantise(1)
+        w_quantise(1, 0)
+        w_quantise(1, 1)
         w_transpose(3, 0)
         w_transpose(3, 1)
         w_empty(3, 0, False)
@@ -370,10 +376,12 @@ def tile_acd_pa_t_kernel(tc, x, q_w, q_b, k_w, k_b, out_0, out_1, out_2):
         empty(0, 1)
         fill_next()
         fill_next()
-        w_quantise(2)
+        w_quantise(2, 0)
+        w_quantise(2, 1)
         fill_next()
         empty(0, 2)
-        w_quantise(3)
+        w_quantise(3, 0)
+        w_quantise(3, 1)
         fill_next()
         empty(0, 3)
         x_quantise(1)

@@ -17,7 +17,7 @@ B, C, N, HEADS, HD = 16, 512, 256, 2, 512
 PACK = 4
 FLOPS = 2 * B * HEADS * 2 * N * C * HD + 2 * B * HEADS * N * N * HD
 LAST_BATCHES = (14, 15)
-GPSIMD_COLUMNS = 200
+GPSIMD_COLUMNS = 192
 VECTOR_COLUMNS = N - GPSIMD_COLUMNS
 NEGATED = 3
 
@@ -275,13 +275,24 @@ def tile_acd_pa_t_kernel(tc, x, q_w, q_b, k_w, k_b, out_0, out_1, out_2):
             nc.tensor.matmul(out=dd, lhsT=ones[:], rhs=dsum_sb[b][:], start=True, stop=True)
 
         def sigmoids(b):
-            diff = dd
             att[b] = work.tile([P, HEADS, N], F32, name="att", bufs=3)
-            nc.scalar.activation(out=att[b][:, 0, :], in_=diff, func=ACT.Sigmoid, scale=inv_sqrt)
-            nc.scalar.activation(out=att[b][:, 1, :], in_=diff, func=ACT.Sigmoid, scale=-inv_sqrt)
+            nc.scalar.activation(out=att[b][:, 0, :], in_=dd, func=ACT.Sigmoid, scale=inv_sqrt)
+            if b in LAST_BATCHES:
+                nc.scalar.activation(out=att[b][:, 1, :], in_=dd, func=ACT.Sigmoid, scale=-inv_sqrt)
 
         def store_att(b):
-            nc.sync.dma_start(out=out_0[b : b + 1].rearrange("o h i j -> o h (i j)"), in_=att[b][0:1, :, :])
+            heads = HEADS if b in LAST_BATCHES else 1
+            nc.sync.dma_start(out=out_0[b : b + 1, 0:heads].rearrange("o h i j -> o h (i j)"), in_=att[b][0:1, 0:heads, :])
+
+        gates = const.tile([B - 2, N], F32, name="gates")
+        others = const.tile([B - 2, N], F32, name="others")
+
+        def load_gates():
+            nc.sync.dma_start(out=gates[:], in_=out_0[0 : B - 2, 0].rearrange("b i j -> b (i j)"))
+
+        def store_others():
+            nc.vector.tensor_scalar(out=others[:], in0=gates[:], scalar1=-1.0, scalar2=1.0, op0=ALU.mult, op1=ALU.add)
+            nc.sync.dma_start(out=out_0[0 : B - 2, 1].rearrange("b i j -> b (i j)"), in_=others[:])
 
         def enhanced_tile(b):
             enhanced[b] = work.tile([P, HEADS, PACK, N], F32, name="enhanced", tag="big%d" % ((b + 1) % 4), bufs=1, align_bytes=64)
@@ -295,19 +306,24 @@ def tile_acd_pa_t_kernel(tc, x, q_w, q_b, k_w, k_b, out_0, out_1, out_2):
                 stop=True,
             )
 
-        def product(engine, b, lo, hi, values, heads):
-            engine.tensor_tensor(
-                out=enhanced[b][:, heads, :, lo:hi],
-                in0=values.unsqueeze(1).to_broadcast([P, heads.stop - heads.start, PACK, hi - lo]),
-                in1=att[b][:, heads, lo:hi].unsqueeze(2).to_broadcast([P, heads.stop - heads.start, PACK, hi - lo]),
-                op=ALU.mult,
-            )
+        def product(engine, b, h, lo, hi, values):
+            if h == 0:
+                engine.tensor_tensor(
+                    out=enhanced[b][:, 0, :, lo:hi],
+                    in0=values,
+                    in1=att[b][:, 0, lo:hi].unsqueeze(1).to_broadcast([P, PACK, hi - lo]),
+                    op=ALU.mult,
+                )
+            else:
+                engine.tensor_tensor(
+                    out=enhanced[b][:, 1, :, lo:hi], in0=values, in1=enhanced[b][:, 0, :, lo:hi], op=ALU.subtract
+                )
 
-        def product_gpsimd(b, heads):
-            product(nc.gpsimd, b, 0, GPSIMD_COLUMNS, x_raw[b][:, :, 0:GPSIMD_COLUMNS], heads)
+        def product_gpsimd(b, h):
+            product(nc.gpsimd, b, h, 0, GPSIMD_COLUMNS, x_raw[b][:, :, 0:GPSIMD_COLUMNS])
 
-        def product_shared(b):
-            product(nc.vector, b, GPSIMD_COLUMNS, N, x_psum, slice(0, HEADS))
+        def product_shared(b, h):
+            product(nc.vector, b, h, GPSIMD_COLUMNS, N, x_psum)
 
         def store_enhanced(b, heads):
             nc.sync.dma_start(
@@ -409,10 +425,12 @@ def tile_acd_pa_t_kernel(tc, x, q_w, q_b, k_w, k_b, out_0, out_1, out_2):
             if 2 <= s < B:
                 head_runs = [slice(0, HEADS)] if s < B - 1 else [slice(h, h + 1) for h in range(HEADS)]
                 enhanced_tile(s - 2)
-                for heads in head_runs:
-                    product_gpsimd(s - 2, heads)
+                for h in range(HEADS):
+                    product_gpsimd(s - 2, h)
             if s >= B:
                 last_products(s - 2)
+            if s == B:
+                store_others()
             if s == B:
                 sim_passes(s - 1, 0)
                 sum_passes(s - 1, 0)
@@ -449,13 +467,17 @@ def tile_acd_pa_t_kernel(tc, x, q_w, q_b, k_w, k_b, out_0, out_1, out_2):
                             scalar_regroup(s, 3)
                     if idx == 2:
                         if s >= 2:
-                            product_shared(s - 2)
+                            product_shared(s - 2, 0)
                         column_sums(s - 1)
                         sigmoids(s - 1)
                         if s + 3 < B:
                             x_regroup(s + 3)
+                    if idx == 4 and s >= 2:
+                        product_shared(s - 2, 1)
                     empty(s, idx)
                     fill_next()
+                if s == B - 1:
+                    load_gates()
                 if s >= 2:
                     for heads in head_runs:
                         store_enhanced(s - 2, heads)

@@ -17,7 +17,7 @@ B, C, N, HEADS, HD = 16, 512, 256, 2, 512
 PACK = 4
 FLOPS = 2 * B * HEADS * 2 * N * C * HD + 2 * B * HEADS * N * N * HD
 LAST_BATCHES = (14, 15)
-GPSIMD_COLUMNS = 192
+GPSIMD_COLUMNS = 184
 VECTOR_COLUMNS = N - GPSIMD_COLUMNS
 NEGATED = 3
 

import math
from contextlib import ExitStack

import concourse.mybir as mybir
from concourse.masks import make_identity

F32 = mybir.dt.float32
BF16 = mybir.dt.bfloat16
U32 = mybir.dt.uint32
U8 = mybir.dt.uint8
FP8X4 = mybir.dt.float8_e4m3fn_x4
ACT = mybir.ActivationFunctionType
ALU = mybir.AluOpType

P = 128
B, C, N, HEADS, HD = 16, 512, 256, 2, 512
PACK = 4
FLOPS = 2 * B * HEADS * 2 * N * C * HD + 2 * B * HEADS * N * N * HD
LAST_BATCHES = (14, 15)
GPSIMD_COLUMNS = 184
VECTOR_COLUMNS = N - GPSIMD_COLUMNS
NEGATED = 3


def tile_acd_pa_t_kernel(tc, x, q_w, q_b, k_w, k_b, out_0, out_1, out_2):
    nc = tc.nc
    inv_sqrt = 1.0 / math.sqrt(HD)
    with ExitStack() as ctx:
        const = ctx.enter_context(tc.tile_pool(name="const", bufs=1))
        work = ctx.enter_context(tc.tile_pool(name="work", bufs=2))
        psum = ctx.enter_context(tc.psum_pool(name="psum", bufs=1))
        ctx.enter_context(tc.manual_schedule())

        w_dram = (q_w[0], k_w[0], q_w[1], k_w[1])
        w_raw = [[const.tile([P, 2, C], BF16, name="w_raw%d_%d" % (m, half)) for half in range(2)] for m in range(4)]
        x_raw = [const.tile([P, PACK, N], BF16, name="x_raw%d" % b) for b in range(B)]
        qb_bf = const.tile([P, HEADS, PACK], BF16, name="qb_bf")
        kb_bf = const.tile([P, HEADS, PACK], BF16, name="kb_bf")

        def load_w(m):
            rows = w_dram[m].rearrange("(p t) c -> p t c", t=PACK)
            for half in range(2):
                nc.sync.dma_start(out=w_raw[m][half][:], in_=rows[:, 2 * half : 2 * half + 2, :])

        def load_x(b):
            nc.sync.dma_start(
                out=x_raw[b][:].rearrange("p j n -> p (j n)"),
                in_=x[b].rearrange("(p j) h w -> p (j h w)", j=PACK),
            )

        load_w(0)
        load_x(0)
        load_w(1)
        with nc.allow_non_contiguous_dma(reason="bias: four neighbouring values to a partition"):
            nc.sync.dma_start(out=qb_bf[:], in_=q_b.rearrange("h (p t) -> p h t", t=PACK))
            nc.sync.dma_start(out=kb_bf[:], in_=k_b.rearrange("h (p t) -> p h t", t=PACK))
        load_w(2)
        load_x(1)
        load_w(3)
        for b in range(2, B):
            load_x(b)

        warm_operand = const.tile([P, 2 * N], BF16, name="warm_operand")
        nc.vector.memset(warm_operand[:], 0.0)
        ident = const.tile([P, P], F32, name="ident")
        make_identity(nc, ident[:])
        ident_bf = const.tile([P, P], BF16, name="ident_bf")
        make_identity(nc, ident_bf[:])
        ones = const.tile([P, P], F32, name="ones")
        nc.vector.memset(ones[:], 1.0)
        warm_in = const.tile([P, 1], F32, name="warm_in")
        warm_out = const.tile([P, 1], F32, name="warm_out")
        nc.vector.memset(warm_in[:], 0.0)
        nc.scalar.activation(out=warm_out[:], in_=warm_in[:], func=ACT.Sigmoid)
        bias_f = const.tile([P, HEADS, 2, PACK], F32, name="bias_f")

        w_codes = [const.tile([P, HD], U32, name="w_codes%d" % m, align_bytes=64) for m in range(4)]
        w_scales = [const.tile([P, HD], U8, name="w_scales%d" % m, align_bytes=64) for m in range(4)]
        w_banks = {}
        w_grouped = {}

        def w_transpose(m, half):
            words = w_raw[m][half][:].bitcast(F32)
            bank = psum.tile([P, 2, 2, P], F32, name="w_bank", tag=("qk" if m % 2 == 1 else "out"), bufs=(4 if m % 2 == 1 else 2))
            for tt in range(2):
                for u in range(2):
                    nc.tensor.transpose(bank[:, tt, u, :], words[:, tt, u : C // 2 : 2], ident[:])
            w_banks[(m, half)] = bank

        def w_empty(m, half, on_vector):
            if half == 0:
                w_grouped[m] = work.tile([P, PACK, P, PACK], BF16, name="w_grouped", bufs=4, align_bytes=64)
            dst = w_grouped[m][:].bitcast(F32)[:, 2 * half : 2 * half + 2, :, :]
            src = w_banks[(m, half)][:].rearrange("p t u d -> p t d u")
            if on_vector:
                nc.vector.tensor_copy(out=dst, in_=src)
            else:
                nc.scalar.copy(out=dst, in_=src)

        def w_quantise(m, half):
            cols = slice(half * 2 * P, (half + 1) * 2 * P)
            nc.vector.quantize_mx(
                out=w_codes[m][:, cols].bitcast(FP8X4),
                scales=w_scales[m][:, cols],
                in_=w_grouped[m][:, 2 * half : 2 * half + 2].rearrange("p t d j -> p (t d j)"),
            )

        def warm_tensor(passes):
            bank = psum.tile([P, 2 * N], F32, name="warm_bank", tag="qk", bufs=4)
            for k in range(passes):
                nc.tensor.matmul(out=bank[:], lhsT=warm_operand[:, 0:P], rhs=warm_operand[:], start=True, stop=True)

        x_grouped = {}
        x_codes = {}
        x_scales = {}

        def x_regroup(b):
            x_grouped[b] = work.tile([P, N, PACK], BF16, name="x_grouped", bufs=3, align_bytes=64)
            nc.scalar.copy(
                out=x_grouped[b][:].rearrange("p (c i) t -> p c t i", i=4),
                in_=x_raw[b][:].rearrange("p t (c i) -> p c t i", i=4),
            )

        def x_quantise(b):
            x_codes[b] = work.tile([P, N], U32, name="x_codes", bufs=4, align_bytes=64)
            x_scales[b] = work.tile([P, N], U8, name="x_scales", bufs=4, align_bytes=64)
            nc.vector.quantize_mx(
                out=x_codes[b][:].bitcast(FP8X4),
                scales=x_scales[b][:],
                in_=x_grouped[b][:].rearrange("p n j -> p (n j)"),
            )

        banks = {}
        qk_grouped = {}
        qk_codes = {}
        qk_scales = {}
        sim_banks = {}
        dsum_sb = {}
        dd_bank = psum.tile([P, 2 * N], F32, name="dd_bank", bufs=1)
        dd = dd_bank[:, 0:N]
        x_bank = psum.tile([P, 2 * N], F32, name="x_bank", bufs=1)
        x_psum = x_bank[:, 0 : PACK * VECTOR_COLUMNS].rearrange("p (j n) -> p j n", j=PACK)
        order = [(b, i) for b in range(B) for i in range(8 if b == 0 else 6)]
        state = {"next": 0}
        sim_sb = {}
        att = {}
        planes = {}
        x_full = {}
        sq_banks = {}
        enhanced = {}

        def fill(b, i):
            m, nh = i // 2, i % 2
            bank = psum.tile([P, PACK, P], F32, name="qk_bank", tag="qk", bufs=4)
            banks[(b, i)] = bank
            cols = slice(nh * P, (nh + 1) * P)
            for t in range(PACK):
                nc.tensor.matmul_mx(
                    out=bank[:, t, :],
                    lhsT=w_codes[m][:, t * P : (t + 1) * P].bitcast(FP8X4),
                    lhsT_scale=w_scales[m][:, t * P : (t + 1) * P],
                    rhs=x_codes[b][:, cols].bitcast(FP8X4),
                    rhs_scale=x_scales[b][:, cols],
                    start=True,
                    stop=True,
                )

        def fill_next():
            k = state["next"]
            if k < len(order):
                fill(order[k][0], order[k][1])
            state["next"] = k + 1

        def grouped_of(b):
            if b not in qk_grouped:
                qk_grouped[b] = work.tile([P, 4, N, PACK], BF16, name="qk_grouped", tag="big%d" % (b % 4), bufs=1, align_bytes=64)
            return qk_grouped[b]

        def scalar_pass(b, m, th):
            bank = psum.tile([P, 2, N], F32, name="sq_bank", tag="out", bufs=2)
            sq_banks[(b, m, th)] = bank
            for tt in range(2):
                t = 2 * th + tt
                nc.tensor.matmul_mx(
                    out=bank[:, tt, :],
                    lhsT=w_codes[m][:, t * P : (t + 1) * P].bitcast(FP8X4),
                    lhsT_scale=w_scales[m][:, t * P : (t + 1) * P],
                    rhs=x_codes[b][:].bitcast(FP8X4),
                    rhs_scale=x_scales[b][:],
                    start=True,
                    stop=True,
                )

        def scalar_planes(b, m, th):
            if th == 0:
                planes[(b, m)] = work.tile([P, PACK, N], BF16, name="planes", bufs=3)
            for tt in range(2):
                t = 2 * th + tt
                nc.scalar.activation(
                    out=planes[(b, m)][:, t, :],
                    in_=sq_banks[(b, m, th)][:, tt, :],
                    func=ACT.Identity,
                    bias=bias_f[:, m // 2, m % 2, t : t + 1],
                    scale=-1.0 if m == NEGATED else 1.0,
                )

        def scalar_regroup(b, m):
            nc.scalar.copy(
                out=grouped_of(b)[:, m].rearrange("p (c i) t -> p c t i", i=4),
                in_=planes[(b, m)][:].rearrange("p t (c i) -> p c t i", i=4),
            )

        def empty(b, i):
            m, nh = i // 2, i % 2
            grouped_of(b)
            sums = banks[(b, i)][:].rearrange("p t c -> p c t")
            bias = bias_f[:, m // 2, m % 2, :].unsqueeze(1).to_broadcast([P, P, PACK])
            dst = qk_grouped[b][:, m, nh * P : (nh + 1) * P, :]
            if m == NEGATED:
                nc.vector.tensor_tensor(out=dst, in0=bias, in1=sums, op=ALU.subtract)
            else:
                nc.vector.tensor_tensor(out=dst, in0=sums, in1=bias, op=ALU.add)

        def qk_quantise(b, first, last):
            if b not in qk_codes:
                qk_codes[b] = work.tile([P, 4 * N], U32, name="qk_codes", align_bytes=64)
                qk_scales[b] = work.tile([P, 4 * N], U8, name="qk_scales", align_bytes=64)
            cols = slice(first * N, (last + 1) * N)
            nc.vector.quantize_mx(
                out=qk_codes[b][:, cols].bitcast(FP8X4),
                scales=qk_scales[b][:, cols],
                in_=qk_grouped[b][:, first : last + 1].rearrange("p m n j -> p (m n j)"),
            )

        def sim_pass(b, h, qt, out, start, stop):
            q0 = 2 * h * N + qt * P
            k0 = (2 * h + 1) * N
            nc.tensor.matmul_mx(
                out=out,
                lhsT=qk_codes[b][:, q0 : q0 + P].bitcast(FP8X4),
                lhsT_scale=qk_scales[b][:, q0 : q0 + P],
                rhs=qk_codes[b][:, k0 : k0 + N].bitcast(FP8X4),
                rhs_scale=qk_scales[b][:, k0 : k0 + N],
                start=start,
                stop=stop,
            )

        def sum_passes(b, h):
            for qt in range(2):
                sim_pass(b, h, qt, dd, h == 0 and qt == 0, h == 1 and qt == 1)

        def sum_empty(b):
            dsum_sb[b] = work.tile([P, N], F32, name="dsum_sb")
            nc.scalar.copy(out=dsum_sb[b][:], in_=dd)

        def sim_passes(b, h):
            sim_banks[(b, h)] = psum.tile([P, 2, N], F32, name="sim_bank", tag="out", bufs=2)
            for qt in range(2):
                sim_pass(b, h, qt, sim_banks[(b, h)][:, qt, :], True, True)

        def sim_empty(b, h):
            bank = sim_banks[(b, h)]
            if h == 0:
                sim_sb[b] = work.tile([P, HEADS, 2, N], F32, name="sim_sb", bufs=3)
            nc.scalar.activation(
                out=sim_sb[b][:, h], in_=bank[:], func=ACT.Copy, scale=(inv_sqrt if h == 0 else -inv_sqrt)
            )
            if h == 1:
                nc.sync.dma_start(
                    out=out_2[b].rearrange("h (qt p) k -> p (h qt) k", p=P),
                    in_=sim_sb[b][:].rearrange("p h qt k -> p (h qt) k"),
                )

        def column_sums(b):
            nc.tensor.matmul(out=dd, lhsT=ones[:], rhs=dsum_sb[b][:], start=True, stop=True)

        def sigmoids(b):
            att[b] = work.tile([P, HEADS, N], F32, name="att", bufs=3)
            nc.scalar.activation(out=att[b][:, 0, :], in_=dd, func=ACT.Sigmoid, scale=inv_sqrt)
            if b in LAST_BATCHES:
                nc.scalar.activation(out=att[b][:, 1, :], in_=dd, func=ACT.Sigmoid, scale=-inv_sqrt)

        def store_att(b):
            heads = HEADS if b in LAST_BATCHES else 1
            nc.sync.dma_start(out=out_0[b : b + 1, 0:heads].rearrange("o h i j -> o h (i j)"), in_=att[b][0:1, 0:heads, :])

        gates = const.tile([B - 2, N], F32, name="gates")
        others = const.tile([B - 2, N], F32, name="others")

        def load_gates():
            nc.sync.dma_start(out=gates[:], in_=out_0[0 : B - 2, 0].rearrange("b i j -> b (i j)"))

        def store_others():
            nc.vector.tensor_scalar(out=others[:], in0=gates[:], scalar1=-1.0, scalar2=1.0, op0=ALU.mult, op1=ALU.add)
            nc.sync.dma_start(out=out_0[0 : B - 2, 1].rearrange("b i j -> b (i j)"), in_=others[:])

        def enhanced_tile(b):
            enhanced[b] = work.tile([P, HEADS, PACK, N], F32, name="enhanced", tag="big%d" % ((b + 1) % 4), bufs=1, align_bytes=64)

        def x_share(b):
            nc.tensor.matmul(
                out=x_psum,
                lhsT=ident_bf[:],
                rhs=x_raw[b][:, :, GPSIMD_COLUMNS:N],
                start=True,
                stop=True,
            )

        def product(engine, b, h, lo, hi, values):
            if h == 0:
                engine.tensor_tensor(
                    out=enhanced[b][:, 0, :, lo:hi],
                    in0=values,
                    in1=att[b][:, 0, lo:hi].unsqueeze(1).to_broadcast([P, PACK, hi - lo]),
                    op=ALU.mult,
                )
            else:
                engine.tensor_tensor(
                    out=enhanced[b][:, 1, :, lo:hi], in0=values, in1=enhanced[b][:, 0, :, lo:hi], op=ALU.subtract
                )

        def product_gpsimd(b, h):
            product(nc.gpsimd, b, h, 0, GPSIMD_COLUMNS, x_raw[b][:, :, 0:GPSIMD_COLUMNS])

        def product_shared(b, h):
            product(nc.vector, b, h, GPSIMD_COLUMNS, N, x_psum)

        def store_enhanced(b, heads):
            nc.sync.dma_start(
                out=out_1[b].rearrange("(h p j) i w -> p h (j i w)", h=HEADS, j=PACK)[:, heads, :],
                in_=enhanced[b][:, heads].rearrange("p h j n -> p h (j n)"),
            )

        def x_to_psum(b):
            x_full[b] = psum.tile([P, PACK, N], BF16, name="x_full", tag="qk", bufs=4)
            for j0 in (0, 2):
                nc.tensor.matmul(
                    out=x_full[b][:, j0 : j0 + 2, :], lhsT=ident_bf[:], rhs=x_raw[b][:, j0 : j0 + 2, :], start=True, stop=True
                )

        def last_products(b):
            enhanced_tile(b)
            for engine, values, h, j0 in (
                (nc.gpsimd, x_raw[b], 1, 2),
                (nc.vector, x_full[b], 0, 0),
                (nc.vector, x_full[b], 0, 2),
                (nc.vector, x_full[b], 1, 0),
            ):
                engine.tensor_tensor(
                    out=enhanced[b][:, h, j0 : j0 + 2, :],
                    in0=values[:, j0 : j0 + 2, :],
                    in1=att[b][:, h, :].unsqueeze(1).to_broadcast([P, 2, N]),
                    op=ALU.mult,
                )
            for h, j0 in ((0, 0), (0, 2), (1, 2), (1, 0)):
                nc.sync.dma_start(
                    out=out_1[b, h * C : (h + 1) * C].rearrange("(p j) i w -> p j (i w)", j=PACK)[:, j0 : j0 + 2, :],
                    in_=enhanced[b][:, h, j0 : j0 + 2, :],
                )

        x_regroup(0)
        warm_tensor(3)
        w_transpose(0, 0)
        w_transpose(0, 1)
        warm_tensor(2)
        w_empty(0, 0, True)
        w_empty(0, 1, True)
        w_quantise(0, 0)
        w_quantise(0, 1)
        x_quantise(0)
        nc.vector.tensor_copy(out=bias_f[:, :, 0, :], in_=qb_bf[:])
        nc.vector.tensor_copy(out=bias_f[:, 0, 1, :], in_=kb_bf[:, 0, :])
        nc.vector.tensor_scalar_mul(out=bias_f[:, 1, 1, :], in0=kb_bf[:, 1, :], scalar1=-1.0)
        w_transpose(1, 0)
        w_transpose(1, 1)
        w_empty(1, 0, False)
        w_empty(1, 1, False)
        w_transpose(2, 0)
        fill_next()
        fill_next()
        w_transpose(2, 1)
        w_empty(2, 0, False)
        w_empty(2, 1, False)
        empty(0, 0)
        w_quantise(1, 0)
        w_quantise(1, 1)
        w_transpose(3, 0)
        w_transpose(3, 1)
        w_empty(3, 0, False)
        w_empty(3, 1, False)
        x_regroup(1)
        empty(0, 1)
        fill_next()
        fill_next()
        w_quantise(2, 0)
        w_quantise(2, 1)
        fill_next()
        empty(0, 2)
        w_quantise(3, 0)
        w_quantise(3, 1)
        fill_next()
        empty(0, 3)
        x_quantise(1)
        x_regroup(2)
        empty(0, 4)
        fill_next()
        fill_next()
        scalar_pass(1, 3, 0)
        scalar_pass(1, 3, 1)
        scalar_planes(1, 3, 0)
        scalar_planes(1, 3, 1)
        x_regroup(3)
        empty(0, 5)
        fill_next()
        fill_next()
        empty(0, 6)
        fill_next()
        empty(0, 7)
        fill_next()
        qk_quantise(0, 0, 1)
        qk_quantise(0, 2, 3)
        x_quantise(2)

        for s in range(1, B + 2):
            if 2 <= s < B:
                head_runs = [slice(0, HEADS)] if s < B - 1 else [slice(h, h + 1) for h in range(HEADS)]
                enhanced_tile(s - 2)
                for h in range(HEADS):
                    product_gpsimd(s - 2, h)
            if s >= B:
                last_products(s - 2)
            if s == B:
                store_others()
            if s == B:
                sim_passes(s - 1, 0)
                sum_passes(s - 1, 0)
                sim_empty(s - 1, 0)
                sum_passes(s - 1, 1)
                sum_empty(s - 1)
                sim_passes(s - 1, 1)
                sim_empty(s - 1, 1)
                x_to_psum(s - 1)
                column_sums(s - 1)
                sigmoids(s - 1)
                store_att(s - 1)
            if s < B:
                for idx in range(6):
                    if idx == 0:
                        if s == B - 1:
                            scalar_regroup(s, 3)
                        sim_passes(s - 1, 0)
                        sim_empty(s - 1, 0)
                        sim_passes(s - 1, 1)
                        sim_empty(s - 1, 1)
                        if s >= 2:
                            x_share(s - 2)
                        sum_passes(s - 1, 0)
                        sum_passes(s - 1, 1)
                        sum_empty(s - 1)
                        if s + 1 < B:
                            scalar_pass(s + 1, 3, 0)
                            scalar_planes(s + 1, 3, 0)
                    if idx == 1:
                        if s + 1 < B:
                            scalar_pass(s + 1, 3, 1)
                            scalar_planes(s + 1, 3, 1)
                            scalar_regroup(s, 3)
                    if idx == 2:
                        if s >= 2:
                            product_shared(s - 2, 0)
                        column_sums(s - 1)
                        sigmoids(s - 1)
                        if s + 3 < B:
                            x_regroup(s + 3)
                    if idx == 4 and s >= 2:
                        product_shared(s - 2, 1)
                    empty(s, idx)
                    fill_next()
                if s == B - 1:
                    load_gates()
                if s >= 2:
                    for heads in head_runs:
                        store_enhanced(s - 2, heads)
                store_att(s - 1)
                qk_quantise(s, 0, 1)
                if s < B - 1:
                    qk_quantise(s, 2, 3)
                else:
                    qk_quantise(s, 3, 3)
                    qk_quantise(s, 2, 2)
                    x_to_psum(s - 1)
                if s + 2 < B:
                    x_quantise(s + 2)
